import numpy as np
import ml_dtypes


def mxq(x, axis, fmt="e4m3"):
    dtype, down = {"e4m3": (ml_dtypes.float8_e4m3fn, 7), "e5m2": (ml_dtypes.float8_e5m2, 14)}[fmt]
    v = np.moveaxis(np.asarray(x, np.float32).astype(ml_dtypes.bfloat16).astype(np.float64), axis, -1)
    blocks = v.reshape(v.shape[:-1] + (-1, 32))
    amax = np.abs(blocks).max(-1, keepdims=True)
    byte = np.maximum(np.where(amax > 0, np.frexp(amax)[1] - 1 + 127, 0) - down, 1)
    scale = np.exp2(byte - 127.0)
    codes = (blocks / scale).astype(np.float32).astype(dtype).astype(np.float64)
    return np.moveaxis((codes * scale).reshape(v.shape), -1, axis)


WIDE = False


def mx_kscale(k):
    if not WIDE:
        return np.ones(k)
    levels = np.array([10, -10, 5, -5, 0])
    a = np.random.permutation(np.resize(levels, k // 512 * 4)).reshape(k // 512, 4)
    idx = np.arange(k)
    return np.exp2(a[idx // 512, idx % 128 // 32])


BF16 = ml_dtypes.bfloat16


def bf(x):
    return np.asarray(x, np.float32).astype(BF16)


def f64(x):
    return np.asarray(x).astype(np.float64)


BS, BLOCK, HID, GAP, G = 256, 512, 1024, 64, 8


def elu(v):
    return np.where(v > 0.0, v, np.exp(np.minimum(v, 0.0)) - 1.0)


def setup_inputs():
    s = mx_kscale(BLOCK)
    s = s / s.max()
    return {"x_blocks": bf((np.random.standard_normal((BS, G, BLOCK)) * s[None, None, :]).reshape(BS, G * BLOCK)),
            "w1": bf(np.random.standard_normal((G, BLOCK, HID)) / np.sqrt(BLOCK) / s[None, :, None]),
            "b1": bf(np.random.standard_normal((G, 1, HID)) * 0.2),
            "w2": bf(np.random.standard_normal((G, HID, BLOCK)) / np.sqrt(HID)),
            "b2": bf(np.random.standard_normal((G, 1, BLOCK)) * 0.2)}


def reference(x_blocks, w1, b1, w2, b2):
    y = f64(x_blocks)
    bs = y.shape[0]
    z = y.reshape(bs, -1, BLOCK).transpose(1, 0, 2)
    h = elu((mxq(z, 2, "e4m3") @ mxq(f64(w1), 1, "e4m3")) + f64(b1))
    h = (mxq(h, 2, "e4m3") @ mxq(f64(w2), 1, "e4m3")) + f64(b2)
    z = h + z
    return z.transpose(1, 0, 2).reshape(bs, -1)

@@ -1,0 +1,268 @@
+from contextlib import ExitStack
+
+import concourse.bass as bass
+import concourse.mybir as mybir
+import concourse.tile as tile
+from concourse.masks import make_identity
+
+F32 = mybir.dt.float32
+BF16 = mybir.dt.bfloat16
+U32 = mybir.dt.uint32
+U8 = mybir.dt.uint8
+FP8X4 = mybir.dt.float8_e4m3fn_x4
+ACT = mybir.ActivationFunctionType
+ALU = mybir.AluOpType
+
+P = 128
+BS = 256
+G = 8
+BLOCK = 512
+HID = 1024
+UNIT = 512
+FLOPS = 2 * BS * BLOCK * HID * G * 2
+
+RAW_BUFS = 3
+V_COLS_W1 = 0
+V_COLS_W2 = 512
+
+
+def tile_blockresmlp_mixerblock_pb_kernel(tc, x_blocks, w1, b1, w2, b2, out):
+    nc = tc.nc
+    with ExitStack() as ctx:
+        const = ctx.enter_context(tc.tile_pool(name="const", bufs=1))
+        rawp = ctx.enter_context(tc.tile_pool(name="rawp", bufs=RAW_BUFS))
+        grp = ctx.enter_context(tc.tile_pool(name="grp", bufs=3))
+        wq = ctx.enter_context(tc.tile_pool(name="wq", bufs=3))
+        actp = ctx.enter_context(tc.tile_pool(name="actp", bufs=2))
+        outp = ctx.enter_context(tc.tile_pool(name="outp", bufs=3))
+        psa = ctx.enter_context(tc.psum_pool(name="psa", bufs=4))
+        psb = ctx.enter_context(tc.psum_pool(name="psb", bufs=4))
+
+        ident_f = const.tile([P, P], F32, name="ident_f")
+        make_identity(nc, ident_f[:])
+        ident_b = const.tile([P, P], BF16, name="ident_b")
+        make_identity(nc, ident_b[:])
+
+        warm_in = const.tile([P, 1], F32, name="warm_in")
+        warm_out = const.tile([P, 1], F32, name="warm_out")
+        nc.vector.memset(warm_in[:], 0.0)
+        nc.scalar.activation(out=warm_out[:], in_=warm_in[:], func=ACT.Exp)
+
+        b1raw = const.tile([P, P], BF16, name="b1raw")
+        nc.vector.memset(b1raw[64:128, :], 0.0)
+        nc.scalar.dma_start(out=b1raw[0:64, :], in_=b1.rearrange("g o (m p) -> (g o m) p", p=P))
+        b2z = const.tile([P, BLOCK], BF16, name="b2z")
+        nc.vector.memset(b2z[:], 0.0)
+        nc.scalar.dma_start(out=b2z[0:G, :], in_=b2.rearrange("g o d -> (g o) d"))
+
+        x_sb = const.tile([P, 2 * G * BLOCK], BF16, name="x_sb")
+        x_view = x_sb[:].rearrange("p (h c) -> p h c", h=2)
+        x_dram = x_blocks.rearrange("(h p) c -> p h c", p=P)
+        x_words = x_sb[:].bitcast(F32)
+
+        def load_x(q):
+            cols = slice(q * 1024, (q + 1) * 1024)
+            nc.sync.dma_start(out=x_view[:, :, cols], in_=x_dram[:, :, cols])
+
+        raw1 = {}
+        raw2 = {}
+
+        def load_w1(g):
+            t = rawp.tile([P, 4, HID], BF16, name="raw1", tag="raw1")
+            nc.sync.dma_start(
+                out=t[:].rearrange("q (u e) n -> q u e n", u=2),
+                in_=w1[g].rearrange("(u q e) n -> q u e n", u=2, q=P, e=2),
+            )
+            raw1[g] = t
+
+        def load_w2(g):
+            t = rawp.tile([P, 8, BLOCK], BF16, name="raw2", tag="raw2")
+            nc.sync.dma_start(out=t[:], in_=w2[g].rearrange("(s p) d -> p s d", p=P))
+            raw2[g] = t
+
+        load_x(0)
+        load_w1(0)
+        load_x(1)
+        load_w2(0)
+        load_x(2)
+        load_x(3)
+        for g in range(1, RAW_BUFS):
+            load_w1(g)
+            load_w2(g)
+
+        b1ps = psa.tile([P, P], BF16, name="b1ps", tag="a")
+        nc.tensor.transpose(out=b1ps[:], in_=b1raw[:], identity=ident_b[:])
+        b1t = const.tile([P, 64], F32, name="b1t")
+        nc.vector.tensor_copy(out=b1t[:], in_=b1ps[:, 0:64])
+
+        zq = {}
+        zs = {}
+        xb = {}
+        w1q = {}
+        w1s = {}
+        w2q = {}
+        w2s = {}
+        hq = {}
+        hs = {}
+
+        def x_path(g):
+            xt = psa.tile([P, 2, BS], F32, name="xt", tag="a")
+            for u in range(2):
+                for h in range(2):
+                    w0 = h * 2048 + 256 * g + 128 * u
+                    nc.tensor.transpose(
+                        out=xt[:, u, h * P : (h + 1) * P],
+                        in_=x_words[:, w0 : w0 + P],
+                        identity=ident_f[:],
+                    )
+            zg = actp.tile([P, 4 * BS], BF16, name="zg", tag="zg", align_bytes=64)
+            nc.scalar.copy(
+                out=zg[:].bitcast(F32).rearrange("p (b u) -> p b u", u=2),
+                in_=xt[:].rearrange("p u b -> p b u"),
+            )
+            zq[g] = actp.tile([P, BS], U32, name="zq", tag="zq", align_bytes=64)
+            zs[g] = actp.tile([P, BS], U8, name="zs", tag="zs", align_bytes=64)
+            nc.vector.quantize_mx(out=zq[g][:].bitcast(FP8X4), scales=zs[g][:], in_=zg[:])
+
+        def resid(g):
+            bb = psb.tile([P, BLOCK], F32, name="bb", tag="b")
+            nc.tensor.matmul(
+                out=bb[:],
+                lhsT=ident_b[:, g : g + 1].to_broadcast([P, P]),
+                rhs=b2z[:],
+                start=True,
+                stop=True,
+            )
+            xb[g] = outp.tile([P, 2, BLOCK], F32, name="xb", tag="xb")
+            for h in range(2):
+                nc.vector.tensor_tensor(
+                    out=xb[g][:, h, :],
+                    in0=bb[:],
+                    in1=x_view[:, h, g * BLOCK : (g + 1) * BLOCK],
+                    op=ALU.add,
+                )
+
+        def regroup(dst, src, v_cols):
+            if v_cols > 0:
+                nc.vector.tensor_copy(
+                    out=dst[:, 0:v_cols, :].rearrange("p (c i) t -> p c t i", i=4),
+                    in_=src[:, :, 0:v_cols].rearrange("p t (c i) -> p c t i", i=4),
+                )
+            if v_cols < UNIT:
+                nc.scalar.copy(
+                    out=dst[:, v_cols:UNIT, :].rearrange("p (c i) t -> p c t i", i=4),
+                    in_=src[:, :, v_cols:UNIT].rearrange("p t (c i) -> p c t i", i=4),
+                )
+
+        def prep(i):
+            g, c = divmod(i, 2)
+            g1 = grp.tile([P, UNIT, 4], BF16, name="g1", tag="g1", align_bytes=64)
+            regroup(g1, raw1[g][:, :, c * UNIT : (c + 1) * UNIT], V_COLS_W1)
+            g2 = grp.tile([P, UNIT, 4], BF16, name="g2", tag="g2", align_bytes=64)
+            regroup(g2, raw2[g][:, 4 * c : 4 * c + 4, :], V_COLS_W2)
+            w1q[i] = wq.tile([P, UNIT], U32, name="w1q", tag="w1q", align_bytes=64)
+            w1s[i] = wq.tile([P, UNIT], U8, name="w1s", tag="w1s", align_bytes=64)
+            nc.vector.quantize_mx(
+                out=w1q[i][:].bitcast(FP8X4),
+                scales=w1s[i][:],
+                in_=g1[:].rearrange("p n t -> p (n t)"),
+            )
+            w2q[i] = wq.tile([P, UNIT], U32, name="w2q", tag="w2q", bufs=4, align_bytes=64)
+            w2s[i] = wq.tile([P, UNIT], U8, name="w2s", tag="w2s", bufs=4, align_bytes=64)
+            nc.vector.quantize_mx(
+                out=w2q[i][:].bitcast(FP8X4),
+                scales=w2s[i][:],
+                in_=g2[:].rearrange("p n t -> p (n t)"),
+            )
+
+        def hidden(i):
+            g, c = divmod(i, 2)
+            banks = [
+                psa.tile([P, 2, BS], F32, name="hp0", tag="a"),
+                psa.tile([P, 2, BS], F32, name="hp1", tag="a"),
+            ]
+            for t in range(4):
+                nc.tensor.matmul_mx(
+                    out=banks[t // 2][:, t % 2, :],
+                    lhsT=w1q[i][:, t * P : (t + 1) * P].bitcast(FP8X4),
+                    lhsT_scale=w1s[i][:, t * P : (t + 1) * P],
+                    rhs=zq[g][:].bitcast(FP8X4),
+                    rhs_scale=zs[g][:],
+                    start=True,
+                    stop=True,
+                )
+            e = actp.tile([P, 4, BS], F32, name="e", tag="e")
+            r = actp.tile([P, 4, BS], F32, name="r", tag="r")
+            for t in range(4):
+                col = 8 * g + 4 * c + t
+                nc.scalar.activation(
+                    out=e[:, t, :],
+                    in_=banks[t // 2][:, t % 2, :],
+                    func=ACT.Exp,
+                    bias=b1t[:, col : col + 1],
+                    scale=1.0,
+                )
+                nc.scalar.activation(
+                    out=r[:, t, :],
+                    in_=banks[t // 2][:, t % 2, :],
+                    func=ACT.Relu,
+                    bias=b1t[:, col : col + 1],
+                    scale=1.0,
+                )
+            hg = actp.tile([P, BS, 4], BF16, name="hg", tag="hg", align_bytes=64)
+            nc.vector.scalar_tensor_tensor(
+                out=hg[:],
+                in0=e[:].rearrange("p t b -> p b t"),
+                scalar=-1.0,
+                in1=r[:].rearrange("p t b -> p b t"),
+                op0=ALU.add,
+                op1=ALU.min,
+            )
+            hq[i] = actp.tile([P, BS], U32, name="hq", tag="hq", bufs=4, align_bytes=64)
+            hs[i] = actp.tile([P, BS], U8, name="hs", tag="hs", bufs=4, align_bytes=64)
+            nc.vector.quantize_mx(
+                out=hq[i][:].bitcast(FP8X4),
+                scales=hs[i][:],
+                in_=hg[:].rearrange("p b t -> p (b t)"),
+            )
+
+        def output(g):
+            for h in range(2):
+                acc = psb.tile([P, BLOCK], F32, name="acc", tag="b")
+                for c in range(2):
+                    i = 2 * g + c
+                    nc.tensor.matmul_mx(
+                        out=acc[:],
+                        lhsT=hq[i][:, h * P : (h + 1) * P].bitcast(FP8X4),
+                        lhsT_scale=hs[i][:, h * P : (h + 1) * P],
+                        rhs=w2q[i][:].bitcast(FP8X4),
+                        rhs_scale=w2s[i][:],
+                        start=(c == 0),
+                        stop=(c == 1),
+                    )
+                res = outp.tile([P, BLOCK], F32, name="res", tag="res", bufs=4)
+                nc.vector.tensor_tensor(out=res[:], in0=acc[:], in1=xb[g][:, h, :], op=ALU.add)
+                nc.sync.dma_start(
+                    out=out[h * P : (h + 1) * P, g * BLOCK : (g + 1) * BLOCK], in_=res[:]
+                )
+
+        x_path(0)
+        prep(0)
+        prep(1)
+        load_w1(RAW_BUFS)
+        load_w2(RAW_BUFS)
+        resid(0)
+        for i in range(2 * G):
+            g, c = divmod(i, 2)
+            j = i + 2
+            if j < 2 * G:
+                prep(j)
+                if j % 2 == 1 and j // 2 + RAW_BUFS < G:
+                    load_w1(j // 2 + RAW_BUFS)
+                    load_w2(j // 2 + RAW_BUFS)
+            if c == 0 and g + 1 < G:
+                x_path(g + 1)
+                resid(g + 1)
+            hidden(i)
+            if c == 1:
+                output(g)

@@ -1,8 +1,6 @@
 from contextlib import ExitStack
 
-import concourse.bass as bass
 import concourse.mybir as mybir
-import concourse.tile as tile
 from concourse.masks import make_identity
 
 F32 = mybir.dt.float32
@@ -19,11 +17,14 @@ G = 8
 BLOCK = 512
 HID = 1024
 UNIT = 512
+NP = 2 * G
 FLOPS = 2 * BS * BLOCK * HID * G * 2
 
+MANUAL = True
 RAW_BUFS = 3
-V_COLS_W1 = 0
-V_COLS_W2 = 512
+V1 = 0
+V2 = 416
+VHEAD = 336
 
 
 def tile_blockresmlp_mixerblock_pb_kernel(tc, x_blocks, w1, b1, w2, b2, out):
@@ -32,11 +33,13 @@ def tile_blockresmlp_mixerblock_pb_kernel(tc, x_blocks, w1, b1, w2, b2, out):
         const = ctx.enter_context(tc.tile_pool(name="const", bufs=1))
         rawp = ctx.enter_context(tc.tile_pool(name="rawp", bufs=RAW_BUFS))
         grp = ctx.enter_context(tc.tile_pool(name="grp", bufs=3))
-        wq = ctx.enter_context(tc.tile_pool(name="wq", bufs=3))
+        wq = ctx.enter_context(tc.tile_pool(name="wq", bufs=2))
         actp = ctx.enter_context(tc.tile_pool(name="actp", bufs=2))
         outp = ctx.enter_context(tc.tile_pool(name="outp", bufs=3))
         psa = ctx.enter_context(tc.psum_pool(name="psa", bufs=4))
-        psb = ctx.enter_context(tc.psum_pool(name="psb", bufs=4))
+        psb = ctx.enter_context(tc.psum_pool(name="psb", bufs=1))
+        if MANUAL:
+            ctx.enter_context(tc.manual_schedule())
 
         ident_f = const.tile([P, P], F32, name="ident_f")
         make_identity(nc, ident_f[:])
@@ -45,24 +48,18 @@ def tile_blockresmlp_mixerblock_pb_kernel(tc, x_blocks, w1, b1, w2, b2, out):
 
         warm_in = const.tile([P, 1], F32, name="warm_in")
         warm_out = const.tile([P, 1], F32, name="warm_out")
+        b1raw = const.tile([P, P], BF16, name="b1raw")
+        b2z = const.tile([P, BLOCK], BF16, name="b2z")
+        nc.vector.memset(b2z[:], 0.0)
+        nc.vector.memset(b1raw[64:128, :], 0.0)
         nc.vector.memset(warm_in[:], 0.0)
         nc.scalar.activation(out=warm_out[:], in_=warm_in[:], func=ACT.Exp)
 
-        b1raw = const.tile([P, P], BF16, name="b1raw")
-        nc.vector.memset(b1raw[64:128, :], 0.0)
-        nc.scalar.dma_start(out=b1raw[0:64, :], in_=b1.rearrange("g o (m p) -> (g o m) p", p=P))
-        b2z = const.tile([P, BLOCK], BF16, name="b2z")
-        nc.vector.memset(b2z[:], 0.0)
-        nc.scalar.dma_start(out=b2z[0:G, :], in_=b2.rearrange("g o d -> (g o) d"))
-
-        x_sb = const.tile([P, 2 * G * BLOCK], BF16, name="x_sb")
-        x_view = x_sb[:].rearrange("p (h c) -> p h c", h=2)
         x_dram = x_blocks.rearrange("(h p) c -> p h c", p=P)
-        x_words = x_sb[:].bitcast(F32)
+        x_sb = [const.tile([P, 2, 2 * BLOCK], BF16, name="x_sb%d" % q) for q in range(G // 2)]
 
         def load_x(q):
-            cols = slice(q * 1024, (q + 1) * 1024)
-            nc.sync.dma_start(out=x_view[:, :, cols], in_=x_dram[:, :, cols])
+            nc.sync.dma_start(out=x_sb[q][:], in_=x_dram[:, :, q * 1024 : (q + 1) * 1024])
 
         raw1 = {}
         raw2 = {}
@@ -80,110 +77,137 @@ def tile_blockresmlp_mixerblock_pb_kernel(tc, x_blocks, w1, b1, w2, b2, out):
             nc.sync.dma_start(out=t[:], in_=w2[g].rearrange("(s p) d -> p s d", p=P))
             raw2[g] = t
 
+        nc.sync.dma_start(out=b1raw[0:64, :], in_=b1.rearrange("g o (m p) -> (g o m) p", p=P))
         load_x(0)
+        nc.sync.dma_start(out=b2z[0:G, :], in_=b2.rearrange("g o d -> (g o) d"))
         load_w1(0)
-        load_x(1)
         load_w2(0)
-        load_x(2)
-        load_x(3)
-        for g in range(1, RAW_BUFS):
+        load_w1(1)
+        load_w2(1)
+        load_x(1)
+        for g in range(2, RAW_BUFS):
             load_w1(g)
             load_w2(g)
-
-        b1ps = psa.tile([P, P], BF16, name="b1ps", tag="a")
-        nc.tensor.transpose(out=b1ps[:], in_=b1raw[:], identity=ident_b[:])
-        b1t = const.tile([P, 64], F32, name="b1t")
-        nc.vector.tensor_copy(out=b1t[:], in_=b1ps[:, 0:64])
+        load_x(2)
+        load_x(3)
 
         zq = {}
         zs = {}
         xb = {}
+        g1 = {}
+        g2 = {}
         w1q = {}
         w1s = {}
         w2q = {}
         w2s = {}
+        hp = {}
+        er = {}
+        hu = {}
+        hg = {}
         hq = {}
         hs = {}
+        acc = {}
 
-        def x_path(g):
-            xt = psa.tile([P, 2, BS], F32, name="xt", tag="a")
+        def x_transposes(g):
+            xt = psb.tile([P, 2, BS], F32, name="xt", tag="xt")
             for u in range(2):
                 for h in range(2):
-                    w0 = h * 2048 + 256 * g + 128 * u
+                    w0 = h * 512 + 256 * (g % 2) + 128 * u
                     nc.tensor.transpose(
                         out=xt[:, u, h * P : (h + 1) * P],
-                        in_=x_words[:, w0 : w0 + P],
+                        in_=x_sb[g // 2][:].rearrange("p h c -> p (h c)").bitcast(F32)[:, w0 : w0 + P],
                         identity=ident_f[:],
                     )
+            return xt
+
+        def x_evac(g, xt):
             zg = actp.tile([P, 4 * BS], BF16, name="zg", tag="zg", align_bytes=64)
             nc.scalar.copy(
                 out=zg[:].bitcast(F32).rearrange("p (b u) -> p b u", u=2),
                 in_=xt[:].rearrange("p u b -> p b u"),
             )
-            zq[g] = actp.tile([P, BS], U32, name="zq", tag="zq", align_bytes=64)
-            zs[g] = actp.tile([P, BS], U8, name="zs", tag="zs", align_bytes=64)
+            return zg
+
+        def x_quant(g, zg):
+            zq[g] = actp.tile([P, BS], U32, name="zq", tag="zq", bufs=3, align_bytes=64)
+            zs[g] = actp.tile([P, BS], U8, name="zs", tag="zs", bufs=3, align_bytes=64)
             nc.vector.quantize_mx(out=zq[g][:].bitcast(FP8X4), scales=zs[g][:], in_=zg[:])
 
-        def resid(g):
-            bb = psb.tile([P, BLOCK], F32, name="bb", tag="b")
+        bbs = {}
+
+        def bias_rows(g):
+            bbs[g] = psb.tile([P, BLOCK], F32, name="bb", tag="bb")
             nc.tensor.matmul(
-                out=bb[:],
+                out=bbs[g][:],
                 lhsT=ident_b[:, g : g + 1].to_broadcast([P, P]),
                 rhs=b2z[:],
                 start=True,
                 stop=True,
             )
-            xb[g] = outp.tile([P, 2, BLOCK], F32, name="xb", tag="xb")
-            for h in range(2):
-                nc.vector.tensor_tensor(
-                    out=xb[g][:, h, :],
-                    in0=bb[:],
-                    in1=x_view[:, h, g * BLOCK : (g + 1) * BLOCK],
-                    op=ALU.add,
-                )
 
-        def regroup(dst, src, v_cols):
-            if v_cols > 0:
-                nc.vector.tensor_copy(
-                    out=dst[:, 0:v_cols, :].rearrange("p (c i) t -> p c t i", i=4),
-                    in_=src[:, :, 0:v_cols].rearrange("p t (c i) -> p c t i", i=4),
-                )
-            if v_cols < UNIT:
-                nc.scalar.copy(
-                    out=dst[:, v_cols:UNIT, :].rearrange("p (c i) t -> p c t i", i=4),
-                    in_=src[:, :, v_cols:UNIT].rearrange("p t (c i) -> p c t i", i=4),
-                )
+        def resid(g, h):
+            if h == 0:
+                xb[g] = outp.tile([P, 2, BLOCK], F32, name="xb", tag="xb")
+            nc.vector.tensor_tensor(
+                out=xb[g][:, h, :],
+                in0=bbs[g][:],
+                in1=x_sb[g // 2][:, h, (g % 2) * BLOCK : (g % 2 + 1) * BLOCK],
+                op=ALU.add,
+            )
 
-        def prep(i):
+        def regroup(eng, dst, src, c0, c1):
+            if c1 <= c0:
+                return
+            o = dst[:, c0:c1, :].rearrange("p (c i) t -> p c t i", i=4)
+            s = src[:, :, c0:c1].rearrange("p t (c i) -> p c t i", i=4)
+            if eng == "v":
+                nc.vector.tensor_copy(out=o, in_=s)
+            else:
+                nc.scalar.copy(out=o, in_=s)
+
+        def regroup_w1(eng, i):
             g, c = divmod(i, 2)
-            g1 = grp.tile([P, UNIT, 4], BF16, name="g1", tag="g1", align_bytes=64)
-            regroup(g1, raw1[g][:, :, c * UNIT : (c + 1) * UNIT], V_COLS_W1)
-            g2 = grp.tile([P, UNIT, 4], BF16, name="g2", tag="g2", align_bytes=64)
-            regroup(g2, raw2[g][:, 4 * c : 4 * c + 4, :], V_COLS_W2)
+            if i not in g1:
+                g1[i] = grp.tile([P, UNIT, 4], BF16, name="g1", tag="g1", align_bytes=64)
+            v = VHEAD if i < 2 else V1
+            c0, c1 = (0, v) if eng == "v" else (v, UNIT)
+            regroup(eng, g1[i], raw1[g][:, :, c * UNIT : (c + 1) * UNIT], c0, c1)
+
+        def regroup_w2(eng, i):
+            g, c = divmod(i, 2)
+            if i not in g2:
+                g2[i] = grp.tile([P, UNIT, 4], BF16, name="g2", tag="g2", align_bytes=64)
+            v = VHEAD if i < 2 else V2
+            c0, c1 = (0, v) if eng == "v" else (v, UNIT)
+            regroup(eng, g2[i], raw2[g][:, 4 * c : 4 * c + 4, :], c0, c1)
+
+        def quant_w1(i):
             w1q[i] = wq.tile([P, UNIT], U32, name="w1q", tag="w1q", align_bytes=64)
             w1s[i] = wq.tile([P, UNIT], U8, name="w1s", tag="w1s", align_bytes=64)
             nc.vector.quantize_mx(
                 out=w1q[i][:].bitcast(FP8X4),
                 scales=w1s[i][:],
-                in_=g1[:].rearrange("p n t -> p (n t)"),
+                in_=g1[i][:].rearrange("p n t -> p (n t)"),
             )
-            w2q[i] = wq.tile([P, UNIT], U32, name="w2q", tag="w2q", bufs=4, align_bytes=64)
-            w2s[i] = wq.tile([P, UNIT], U8, name="w2s", tag="w2s", bufs=4, align_bytes=64)
+
+        def quant_w2(i):
+            w2q[i] = wq.tile([P, UNIT], U32, name="w2q", tag="w2q", bufs=5, align_bytes=64)
+            w2s[i] = wq.tile([P, UNIT], U8, name="w2s", tag="w2s", bufs=5, align_bytes=64)
             nc.vector.quantize_mx(
                 out=w2q[i][:].bitcast(FP8X4),
                 scales=w2s[i][:],
-                in_=g2[:].rearrange("p n t -> p (n t)"),
+                in_=g2[i][:].rearrange("p n t -> p (n t)"),
             )
 
-        def hidden(i):
-            g, c = divmod(i, 2)
-            banks = [
+        def mm1(i):
+            g = i // 2
+            hp[i] = [
                 psa.tile([P, 2, BS], F32, name="hp0", tag="a"),
                 psa.tile([P, 2, BS], F32, name="hp1", tag="a"),
             ]
             for t in range(4):
                 nc.tensor.matmul_mx(
-                    out=banks[t // 2][:, t % 2, :],
+                    out=hp[i][t // 2][:, t % 2, :],
                     lhsT=w1q[i][:, t * P : (t + 1) * P].bitcast(FP8X4),
                     lhsT_scale=w1s[i][:, t * P : (t + 1) * P],
                     rhs=zq[g][:].bitcast(FP8X4),
@@ -191,48 +215,54 @@ def tile_blockresmlp_mixerblock_pb_kernel(tc, x_blocks, w1, b1, w2, b2, out):
                     start=True,
                     stop=True,
                 )
-            e = actp.tile([P, 4, BS], F32, name="e", tag="e")
-            r = actp.tile([P, 4, BS], F32, name="r", tag="r")
+
+        def exp_relu(i):
+            e = actp.tile([P, 4, BS], F32, name="e", tag="e", bufs=3)
+            r = actp.tile([P, 4, BS], F32, name="r", tag="r", bufs=3)
             for t in range(4):
-                col = 8 * g + 4 * c + t
-                nc.scalar.activation(
-                    out=e[:, t, :],
-                    in_=banks[t // 2][:, t % 2, :],
-                    func=ACT.Exp,
-                    bias=b1t[:, col : col + 1],
-                    scale=1.0,
-                )
-                nc.scalar.activation(
-                    out=r[:, t, :],
-                    in_=banks[t // 2][:, t % 2, :],
-                    func=ACT.Relu,
-                    bias=b1t[:, col : col + 1],
-                    scale=1.0,
-                )
-            hg = actp.tile([P, BS, 4], BF16, name="hg", tag="hg", align_bytes=64)
+                col = 4 * i + t
+                for dst, func in ((e, ACT.Exp), (r, ACT.Relu)):
+                    nc.scalar.activation(
+                        out=dst[:, t, :],
+                        in_=hp[i][t // 2][:, t % 2, :],
+                        func=func,
+                        bias=b1t[:, col : col + 1],
+                        scale=1.0,
+                    )
+            er[i] = (e, r)
+
+        def elu(i):
+            e, r = er[i]
+            hu[i] = actp.tile([P, 4, BS], BF16, name="hu", tag="hu")
             nc.vector.scalar_tensor_tensor(
-                out=hg[:],
-                in0=e[:].rearrange("p t b -> p b t"),
+                out=hu[i][:].rearrange("p t b -> p (t b)"),
+                in0=e[:].rearrange("p t b -> p (t b)"),
                 scalar=-1.0,
-                in1=r[:].rearrange("p t b -> p b t"),
+                in1=r[:].rearrange("p t b -> p (t b)"),
                 op0=ALU.add,
                 op1=ALU.min,
             )
+
+        def regroup_h(i):
+            hg[i] = actp.tile([P, BS, 4], BF16, name="hg", tag="hg", align_bytes=64)
+            regroup("v", hg[i], hu[i], 0, BS)
+
+        def quant_h(i):
             hq[i] = actp.tile([P, BS], U32, name="hq", tag="hq", bufs=4, align_bytes=64)
             hs[i] = actp.tile([P, BS], U8, name="hs", tag="hs", bufs=4, align_bytes=64)
             nc.vector.quantize_mx(
                 out=hq[i][:].bitcast(FP8X4),
                 scales=hs[i][:],
-                in_=hg[:].rearrange("p b t -> p (b t)"),
+                in_=hg[i][:].rearrange("p b t -> p (b t)"),
             )
 
-        def output(g):
+        def mm2(g):
             for h in range(2):
-                acc = psb.tile([P, BLOCK], F32, name="acc", tag="b")
+                acc[(g, h)] = psb.tile([P, BLOCK], F32, name="acc", tag="acc", bufs=2)
                 for c in range(2):
                     i = 2 * g + c
                     nc.tensor.matmul_mx(
-                        out=acc[:],
+                        out=acc[(g, h)][:],
                         lhsT=hq[i][:, h * P : (h + 1) * P].bitcast(FP8X4),
                         lhsT_scale=hs[i][:, h * P : (h + 1) * P],
                         rhs=w2q[i][:].bitcast(FP8X4),
@@ -240,29 +270,77 @@ def tile_blockresmlp_mixerblock_pb_kernel(tc, x_blocks, w1, b1, w2, b2, out):
                         start=(c == 0),
                         stop=(c == 1),
                     )
+
+        def finish(g):
+            for h in range(2):
                 res = outp.tile([P, BLOCK], F32, name="res", tag="res", bufs=4)
-                nc.vector.tensor_tensor(out=res[:], in0=acc[:], in1=xb[g][:, h, :], op=ALU.add)
+                nc.vector.tensor_tensor(
+                    out=res[:], in0=acc[(g, h)][:], in1=xb[g][:, h, :], op=ALU.add
+                )
                 nc.sync.dma_start(
                     out=out[h * P : (h + 1) * P, g * BLOCK : (g + 1) * BLOCK], in_=res[:]
                 )
 
-        x_path(0)
-        prep(0)
-        prep(1)
-        load_w1(RAW_BUFS)
-        load_w2(RAW_BUFS)
-        resid(0)
-        for i in range(2 * G):
-            g, c = divmod(i, 2)
-            j = i + 2
-            if j < 2 * G:
-                prep(j)
-                if j % 2 == 1 and j // 2 + RAW_BUFS < G:
-                    load_w1(j // 2 + RAW_BUFS)
-                    load_w2(j // 2 + RAW_BUFS)
-            if c == 0 and g + 1 < G:
-                x_path(g + 1)
-                resid(g + 1)
-            hidden(i)
-            if c == 1:
-                output(g)
+        xt0 = x_transposes(0)
+        b1ps = psb.tile([P, P], BF16, name="b1ps", tag="acc", bufs=2)
+        nc.tensor.transpose(out=b1ps[:], in_=b1raw[:], identity=ident_b[:])
+        bias_rows(0)
+        zg0 = x_evac(0, xt0)
+        x_quant(0, zg0)
+        b1t = const.tile([P, 64], F32, name="b1t")
+        nc.vector.tensor_copy(out=b1t[:], in_=b1ps[:, 0:64])
+        xt1 = x_transposes(1)
+        for eng in ("v", "s"):
+            regroup_w1(eng, 0)
+            regroup_w1(eng, 1)
+        quant_w1(0)
+        mm1(0)
+        zg1 = x_evac(1, xt1)
+        x_quant(1, zg1)
+        for eng in ("v", "s"):
+            regroup_w2(eng, 0)
+            regroup_w2(eng, 1)
+        quant_w2(0)
+        if RAW_BUFS < G:
+            load_w1(RAW_BUFS)
+            load_w2(RAW_BUFS)
+
+        xts = {}
+        for s in range(NP + 3):
+            even = s % 2 == 0
+            p = s - 1
+            has_p = 0 <= p < NP
+            if s + 1 < NP:
+                quant_w1(s + 1)
+                mm1(s + 1)
+                quant_w2(s + 1)
+            if not even and (s + 3) // 2 < G:
+                xts[(s + 3) // 2] = x_transposes((s + 3) // 2)
+            if s < NP:
+                exp_relu(s)
+            if even and s // 2 < G:
+                resid(s // 2, 0)
+            if has_p:
+                elu(p)
+                regroup_h(p)
+            if s + 2 < NP:
+                regroup_w1("v", s + 2)
+                regroup_w2("v", s + 2)
+                regroup_w1("s", s + 2)
+                regroup_w2("s", s + 2)
+                if not even and (s + 2) // 2 + RAW_BUFS < G:
+                    load_w1((s + 2) // 2 + RAW_BUFS)
+                    load_w2((s + 2) // 2 + RAW_BUFS)
+            if not even and 0 <= (s - 3) // 2 < G:
+                finish((s - 3) // 2)
+            if has_p:
+                quant_h(p)
+                if even:
+                    mm2(s // 2 - 1)
+            if even and s // 2 < G:
+                resid(s // 2, 1)
+                if s // 2 + 1 < G:
+                    bias_rows(s // 2 + 1)
+                if 2 <= s // 2 + 1 < G:
+                    zg = x_evac(s // 2 + 1, xts[s // 2 + 1])
+                    x_quant(s // 2 + 1, zg)

@@ -23,7 +23,7 @@ FLOPS = 2 * BS * BLOCK * HID * G * 2
 MANUAL = True
 RAW_BUFS = 3
 V1 = 0
-V2 = 416
+V2 = 512
 VHEAD = 336
 
 

@@ -25,6 +25,7 @@ RAW_BUFS = 3
 V1 = 0
 V2 = 512
 VHEAD = 336
+GA = 3
 
 
 def tile_blockresmlp_mixerblock_pb_kernel(tc, x_blocks, w1, b1, w2, b2, out):
@@ -145,6 +146,28 @@ def tile_blockresmlp_mixerblock_pb_kernel(tc, x_blocks, w1, b1, w2, b2, out):
                 stop=True,
             )
 
+        def resid_pe(g, h):
+            bbs[(g, h)] = psb.tile([P, BLOCK], F32, name="bx", tag="bb")
+            nc.tensor.matmul(
+                out=bbs[(g, h)][:],
+                lhsT=ident_b[:, g : g + 1].to_broadcast([P, P]),
+                rhs=b2z[:],
+                start=True,
+                stop=False,
+            )
+            nc.tensor.matmul(
+                out=bbs[(g, h)][:],
+                lhsT=ident_b[:],
+                rhs=x_sb[g // 2][:, h, (g % 2) * BLOCK : (g % 2 + 1) * BLOCK],
+                start=False,
+                stop=True,
+            )
+
+        def resid_s(g, h):
+            if h == 0:
+                xb[g] = outp.tile([P, 2, BLOCK], F32, name="xb", tag="xb")
+            nc.scalar.copy(out=xb[g][:, h, :], in_=bbs[(g, h)][:])
+
         def resid(g, h):
             if h == 0:
                 xb[g] = outp.tile([P, 2, BLOCK], F32, name="xb", tag="xb")
@@ -256,20 +279,20 @@ def tile_blockresmlp_mixerblock_pb_kernel(tc, x_blocks, w1, b1, w2, b2, out):
                 in_=hg[i][:].rearrange("p b t -> p (b t)"),
             )
 
-        def mm2(g):
+        def mm2(g, c):
+            i = 2 * g + c
             for h in range(2):
-                acc[(g, h)] = psb.tile([P, BLOCK], F32, name="acc", tag="acc", bufs=2)
-                for c in range(2):
-                    i = 2 * g + c
-                    nc.tensor.matmul_mx(
-                        out=acc[(g, h)][:],
-                        lhsT=hq[i][:, h * P : (h + 1) * P].bitcast(FP8X4),
-                        lhsT_scale=hs[i][:, h * P : (h + 1) * P],
-                        rhs=w2q[i][:].bitcast(FP8X4),
-                        rhs_scale=w2s[i][:],
-                        start=(c == 0),
-                        stop=(c == 1),
-                    )
+                if c == 0:
+                    acc[(g, h)] = psb.tile([P, BLOCK], F32, name="acc", tag="acc", bufs=2)
+                nc.tensor.matmul_mx(
+                    out=acc[(g, h)][:],
+                    lhsT=hq[i][:, h * P : (h + 1) * P].bitcast(FP8X4),
+                    lhsT_scale=hs[i][:, h * P : (h + 1) * P],
+                    rhs=w2q[i][:].bitcast(FP8X4),
+                    rhs_scale=w2s[i][:],
+                    start=(c == 0),
+                    stop=(c == 1),
+                )
 
         def finish(g):
             for h in range(2):
@@ -310,6 +333,7 @@ def tile_blockresmlp_mixerblock_pb_kernel(tc, x_blocks, w1, b1, w2, b2, out):
             even = s % 2 == 0
             p = s - 1
             has_p = 0 <= p < NP
+            gb = s // 2
             if s + 1 < NP:
                 quant_w1(s + 1)
                 mm1(s + 1)
@@ -318,8 +342,8 @@ def tile_blockresmlp_mixerblock_pb_kernel(tc, x_blocks, w1, b1, w2, b2, out):
                 xts[(s + 3) // 2] = x_transposes((s + 3) // 2)
             if s < NP:
                 exp_relu(s)
-            if even and s // 2 < G:
-                resid(s // 2, 0)
+            if even and gb < GA:
+                resid(gb, 0)
             if has_p:
                 elu(p)
                 regroup_h(p)
@@ -335,12 +359,15 @@ def tile_blockresmlp_mixerblock_pb_kernel(tc, x_blocks, w1, b1, w2, b2, out):
                 finish((s - 3) // 2)
             if has_p:
                 quant_h(p)
-                if even:
-                    mm2(s // 2 - 1)
-            if even and s // 2 < G:
-                resid(s // 2, 1)
-                if s // 2 + 1 < G:
-                    bias_rows(s // 2 + 1)
-                if 2 <= s // 2 + 1 < G:
-                    zg = x_evac(s // 2 + 1, xts[s // 2 + 1])
-                    x_quant(s // 2 + 1, zg)
+                mm2(p // 2, p % 2)
+            if even and gb < GA:
+                resid(gb, 1)
+                if gb + 1 < GA:
+                    bias_rows(gb + 1)
+            if GA <= gb < G:
+                resid_s(gb, s % 2)
+            if GA <= (s + 1) // 2 < G:
+                resid_pe((s + 1) // 2, (s + 1) % 2)
+            if even and 2 <= gb + 1 < G:
+                zg = x_evac(gb + 1, xts[gb + 1])
+                x_quant(gb + 1, zg)

@@ -20,12 +20,12 @@ UNIT = 512
 NP = 2 * G
 FLOPS = 2 * BS * BLOCK * HID * G * 2
 
-MANUAL = True
-RAW_BUFS = 3
+RAW_BUFS = 6
 V1 = 0
 V2 = 512
 VHEAD = 336
 GA = 3
+SPLIT_LAST = True
 
 
 def tile_blockresmlp_mixerblock_pb_kernel(tc, x_blocks, w1, b1, w2, b2, out):
@@ -39,61 +39,74 @@ def tile_blockresmlp_mixerblock_pb_kernel(tc, x_blocks, w1, b1, w2, b2, out):
         outp = ctx.enter_context(tc.tile_pool(name="outp", bufs=3))
         psa = ctx.enter_context(tc.psum_pool(name="psa", bufs=4))
         psb = ctx.enter_context(tc.psum_pool(name="psb", bufs=1))
-        if MANUAL:
-            ctx.enter_context(tc.manual_schedule())
+        ctx.enter_context(tc.manual_schedule())
 
         ident_f = const.tile([P, P], F32, name="ident_f")
         make_identity(nc, ident_f[:])
         ident_b = const.tile([P, P], BF16, name="ident_b")
         make_identity(nc, ident_b[:])
-
         warm_in = const.tile([P, 1], F32, name="warm_in")
         warm_out = const.tile([P, 1], F32, name="warm_out")
         b1raw = const.tile([P, P], BF16, name="b1raw")
         b2z = const.tile([P, BLOCK], BF16, name="b2z")
+        b1t = const.tile([P, 64], F32, name="b1t")
         nc.vector.memset(b2z[:], 0.0)
         nc.vector.memset(b1raw[64:128, :], 0.0)
         nc.vector.memset(warm_in[:], 0.0)
         nc.scalar.activation(out=warm_out[:], in_=warm_in[:], func=ACT.Exp)
 
         x_dram = x_blocks.rearrange("(h p) c -> p h c", p=P)
-        x_sb = [const.tile([P, 2, 2 * BLOCK], BF16, name="x_sb%d" % q) for q in range(G // 2)]
-
-        def load_x(q):
-            nc.sync.dma_start(out=x_sb[q][:], in_=x_dram[:, :, q * 1024 : (q + 1) * 1024])
-
+        x_sb = [const.tile([P, 2, BLOCK], BF16, name="x_sb%d" % g) for g in range(G)]
         raw1 = {}
         raw2 = {}
 
-        def load_w1(g):
-            t = rawp.tile([P, 4, HID], BF16, name="raw1", tag="raw1")
-            nc.sync.dma_start(
-                out=t[:].rearrange("q (u e) n -> q u e n", u=2),
-                in_=w1[g].rearrange("(u q e) n -> q u e n", u=2, q=P, e=2),
-            )
-            raw1[g] = t
+        def load(kind, i):
+            g, c = divmod(i, 2)
+            if kind == "b1":
+                nc.sync.dma_start(
+                    out=b1raw[0:64, :], in_=b1.rearrange("g o (m p) -> (g o m) p", p=P)
+                )
+            elif kind == "b2":
+                nc.sync.dma_start(out=b2z[0:G, :], in_=b2.rearrange("g o d -> (g o) d"))
+            elif kind == "x":
+                nc.sync.dma_start(out=x_sb[i][:], in_=x_dram[:, :, i * BLOCK : (i + 1) * BLOCK])
+            elif kind == "w1":
+                raw1[i] = rawp.tile([P, 4, UNIT], BF16, name="raw1", tag="raw1")
+                for u in range(2):
+                    nc.sync.dma_start(
+                        out=raw1[i][:, 2 * u : 2 * u + 2, :],
+                        in_=w1[g][256 * u : 256 * (u + 1), c * UNIT : (c + 1) * UNIT].rearrange(
+                            "(q e) n -> q e n", e=2
+                        ),
+                    )
+            else:
+                raw2[i] = rawp.tile([P, 4, UNIT], BF16, name="raw2", tag="raw2")
+                nc.sync.dma_start(
+                    out=raw2[i][:],
+                    in_=w2[g][c * UNIT : (c + 1) * UNIT, :].rearrange("(t p) d -> p t d", p=P),
+                )
 
-        def load_w2(g):
-            t = rawp.tile([P, 8, BLOCK], BF16, name="raw2", tag="raw2")
-            nc.sync.dma_start(out=t[:], in_=w2[g].rearrange("(s p) d -> p s d", p=P))
-            raw2[g] = t
+        order = [("b1", 0), ("b2", 0), ("x", 0), ("w1", 0), ("w2", 0), ("w1", 1), ("x", 1), ("w2", 1)]
+        for i in range(2, NP):
+            order.append(("w1", i))
+            order.append(("w2", i))
+            if i % 2 == 0 and i // 2 + 1 < G:
+                order.append(("x", i // 2 + 1))
+        issued = [0]
 
-        nc.sync.dma_start(out=b1raw[0:64, :], in_=b1.rearrange("g o (m p) -> (g o m) p", p=P))
-        load_x(0)
-        nc.sync.dma_start(out=b2z[0:G, :], in_=b2.rearrange("g o d -> (g o) d"))
-        load_w1(0)
-        load_w2(0)
-        load_w1(1)
-        load_w2(1)
-        load_x(1)
-        for g in range(2, RAW_BUFS):
-            load_w1(g)
-            load_w2(g)
-        load_x(2)
-        load_x(3)
+        def issue_loads(done):
+            while issued[0] < len(order):
+                kind, i = order[issued[0]]
+                if kind in ("w1", "w2") and i - RAW_BUFS > done:
+                    break
+                load(kind, i)
+                issued[0] += 1
 
+        xts = {}
+        zgs = {}
         zq = {}
         zs = {}
+        bbs = {}
         xb = {}
         g1 = {}
         g2 = {}
@@ -110,73 +123,57 @@ def tile_blockresmlp_mixerblock_pb_kernel(tc, x_blocks, w1, b1, w2, b2, out):
         acc = {}
 
         def x_transposes(g):
-            xt = psb.tile([P, 2, BS], F32, name="xt", tag="xt")
+            xts[g] = psb.tile([P, 2, BS], F32, name="xt", tag="xt")
+            words = x_sb[g][:].rearrange("p h c -> p (h c)").bitcast(F32)
             for u in range(2):
                 for h in range(2):
-                    w0 = h * 512 + 256 * (g % 2) + 128 * u
+                    w0 = h * 256 + 128 * u
                     nc.tensor.transpose(
-                        out=xt[:, u, h * P : (h + 1) * P],
-                        in_=x_sb[g // 2][:].rearrange("p h c -> p (h c)").bitcast(F32)[:, w0 : w0 + P],
+                        out=xts[g][:, u, h * P : (h + 1) * P],
+                        in_=words[:, w0 : w0 + P],
                         identity=ident_f[:],
                     )
-            return xt
 
-        def x_evac(g, xt):
-            zg = actp.tile([P, 4 * BS], BF16, name="zg", tag="zg", align_bytes=64)
+        def x_evac(g):
+            zgs[g] = actp.tile([P, 4 * BS], BF16, name="zg", tag="zg", align_bytes=64)
             nc.scalar.copy(
-                out=zg[:].bitcast(F32).rearrange("p (b u) -> p b u", u=2),
-                in_=xt[:].rearrange("p u b -> p b u"),
+                out=zgs[g][:].bitcast(F32).rearrange("p (b u) -> p b u", u=2),
+                in_=xts[g][:].rearrange("p u b -> p b u"),
             )
-            return zg
 
-        def x_quant(g, zg):
+        def x_quant(g):
             zq[g] = actp.tile([P, BS], U32, name="zq", tag="zq", bufs=3, align_bytes=64)
             zs[g] = actp.tile([P, BS], U8, name="zs", tag="zs", bufs=3, align_bytes=64)
-            nc.vector.quantize_mx(out=zq[g][:].bitcast(FP8X4), scales=zs[g][:], in_=zg[:])
+            nc.vector.quantize_mx(out=zq[g][:].bitcast(FP8X4), scales=zs[g][:], in_=zgs[g][:])
 
-        bbs = {}
-
-        def bias_rows(g):
-            bbs[g] = psb.tile([P, BLOCK], F32, name="bb", tag="bb")
+        def bias_rows(key, g, stop):
+            bbs[key] = psb.tile([P, BLOCK], F32, name="bb", tag="bb")
             nc.tensor.matmul(
-                out=bbs[g][:],
+                out=bbs[key][:],
                 lhsT=ident_b[:, g : g + 1].to_broadcast([P, P]),
                 rhs=b2z[:],
                 start=True,
-                stop=True,
+                stop=stop,
+            )
+
+        def resid_tile(g):
+            if g not in xb:
+                xb[g] = outp.tile([P, 2, BLOCK], F32, name="xb", tag="xb")
+            return xb[g]
+
+        def resid_v(g, h):
+            nc.vector.tensor_tensor(
+                out=resid_tile(g)[:, h, :], in0=bbs[g][:], in1=x_sb[g][:, h, :], op=ALU.add
             )
 
         def resid_pe(g, h):
-            bbs[(g, h)] = psb.tile([P, BLOCK], F32, name="bx", tag="bb")
+            bias_rows((g, h), g, False)
             nc.tensor.matmul(
-                out=bbs[(g, h)][:],
-                lhsT=ident_b[:, g : g + 1].to_broadcast([P, P]),
-                rhs=b2z[:],
-                start=True,
-                stop=False,
-            )
-            nc.tensor.matmul(
-                out=bbs[(g, h)][:],
-                lhsT=ident_b[:],
-                rhs=x_sb[g // 2][:, h, (g % 2) * BLOCK : (g % 2 + 1) * BLOCK],
-                start=False,
-                stop=True,
+                out=bbs[(g, h)][:], lhsT=ident_b[:], rhs=x_sb[g][:, h, :], start=False, stop=True
             )
 
         def resid_s(g, h):
-            if h == 0:
-                xb[g] = outp.tile([P, 2, BLOCK], F32, name="xb", tag="xb")
-            nc.scalar.copy(out=xb[g][:, h, :], in_=bbs[(g, h)][:])
-
-        def resid(g, h):
-            if h == 0:
-                xb[g] = outp.tile([P, 2, BLOCK], F32, name="xb", tag="xb")
-            nc.vector.tensor_tensor(
-                out=xb[g][:, h, :],
-                in0=bbs[g][:],
-                in1=x_sb[g // 2][:, h, (g % 2) * BLOCK : (g % 2 + 1) * BLOCK],
-                op=ALU.add,
-            )
+            nc.scalar.copy(out=resid_tile(g)[:, h, :], in_=bbs[(g, h)][:])
 
         def regroup(eng, dst, src, c0, c1):
             if c1 <= c0:
@@ -188,38 +185,21 @@ def tile_blockresmlp_mixerblock_pb_kernel(tc, x_blocks, w1, b1, w2, b2, out):
             else:
                 nc.scalar.copy(out=o, in_=s)
 
-        def regroup_w1(eng, i):
-            g, c = divmod(i, 2)
+        def regroup_w(eng, kind, i):
             if i not in g1:
-                g1[i] = grp.tile([P, UNIT, 4], BF16, name="g1", tag="g1", align_bytes=64)
-            v = VHEAD if i < 2 else V1
+                g1[i] = grp.tile([P, 2, UNIT, 4], BF16, name="gw", tag="gw", align_bytes=64)
+            raws, share = (raw1, V1) if kind == 1 else (raw2, V2)
+            v = VHEAD if i < 2 else share
             c0, c1 = (0, v) if eng == "v" else (v, UNIT)
-            regroup(eng, g1[i], raw1[g][:, :, c * UNIT : (c + 1) * UNIT], c0, c1)
+            regroup(eng, g1[i][:, kind - 1, :, :], raws[i], c0, c1)
 
-        def regroup_w2(eng, i):
-            g, c = divmod(i, 2)
-            if i not in g2:
-                g2[i] = grp.tile([P, UNIT, 4], BF16, name="g2", tag="g2", align_bytes=64)
-            v = VHEAD if i < 2 else V2
-            c0, c1 = (0, v) if eng == "v" else (v, UNIT)
-            regroup(eng, g2[i], raw2[g][:, 4 * c : 4 * c + 4, :], c0, c1)
-
-        def quant_w1(i):
-            w1q[i] = wq.tile([P, UNIT], U32, name="w1q", tag="w1q", align_bytes=64)
-            w1s[i] = wq.tile([P, UNIT], U8, name="w1s", tag="w1s", align_bytes=64)
+        def quant_w(i):
+            w1q[i] = wq.tile([P, 2, UNIT], U32, name="wc", tag="wc", bufs=5, align_bytes=64)
+            w1s[i] = wq.tile([P, 2, UNIT], U8, name="ws", tag="ws", bufs=5, align_bytes=64)
             nc.vector.quantize_mx(
-                out=w1q[i][:].bitcast(FP8X4),
-                scales=w1s[i][:],
-                in_=g1[i][:].rearrange("p n t -> p (n t)"),
-            )
-
-        def quant_w2(i):
-            w2q[i] = wq.tile([P, UNIT], U32, name="w2q", tag="w2q", bufs=5, align_bytes=64)
-            w2s[i] = wq.tile([P, UNIT], U8, name="w2s", tag="w2s", bufs=5, align_bytes=64)
-            nc.vector.quantize_mx(
-                out=w2q[i][:].bitcast(FP8X4),
-                scales=w2s[i][:],
-                in_=g2[i][:].rearrange("p n t -> p (n t)"),
+                out=w1q[i][:].rearrange("p k n -> p (k n)").bitcast(FP8X4),
+                scales=w1s[i][:].rearrange("p k n -> p (k n)"),
+                in_=g1[i][:].rearrange("p k n t -> p (k n t)"),
             )
 
         def mm1(i):
@@ -231,143 +211,156 @@ def tile_blockresmlp_mixerblock_pb_kernel(tc, x_blocks, w1, b1, w2, b2, out):
             for t in range(4):
                 nc.tensor.matmul_mx(
                     out=hp[i][t // 2][:, t % 2, :],
-                    lhsT=w1q[i][:, t * P : (t + 1) * P].bitcast(FP8X4),
-                    lhsT_scale=w1s[i][:, t * P : (t + 1) * P],
+                    lhsT=w1q[i][:, 0, t * P : (t + 1) * P].bitcast(FP8X4),
+                    lhsT_scale=w1s[i][:, 0, t * P : (t + 1) * P],
                     rhs=zq[g][:].bitcast(FP8X4),
                     rhs_scale=zs[g][:],
                     start=True,
                     stop=True,
                 )
 
-        def exp_relu(i):
-            e = actp.tile([P, 4, BS], F32, name="e", tag="e", bufs=3)
-            r = actp.tile([P, 4, BS], F32, name="r", tag="r", bufs=3)
+        def exp_relu(i, b0, b1_):
+            if i not in er:
+                er[i] = (
+                    actp.tile([P, 4, BS], F32, name="e", tag="e", bufs=3),
+                    actp.tile([P, 4, BS], F32, name="r", tag="r", bufs=3),
+                )
             for t in range(4):
                 col = 4 * i + t
-                for dst, func in ((e, ACT.Exp), (r, ACT.Relu)):
+                for dst, func in zip(er[i], (ACT.Exp, ACT.Relu)):
                     nc.scalar.activation(
-                        out=dst[:, t, :],
-                        in_=hp[i][t // 2][:, t % 2, :],
+                        out=dst[:, t, b0:b1_],
+                        in_=hp[i][t // 2][:, t % 2, b0:b1_],
                         func=func,
                         bias=b1t[:, col : col + 1],
                         scale=1.0,
                     )
-            er[i] = (e, r)
 
-        def elu(i):
+        def elu(i, b0, b1_):
             e, r = er[i]
-            hu[i] = actp.tile([P, 4, BS], BF16, name="hu", tag="hu")
+            if i not in hg:
+                hg[i] = actp.tile([P, BS, 4], BF16, name="hg", tag="hg", align_bytes=64)
             nc.vector.scalar_tensor_tensor(
-                out=hu[i][:].rearrange("p t b -> p (t b)"),
-                in0=e[:].rearrange("p t b -> p (t b)"),
+                out=hg[i][:, b0:b1_, :],
+                in0=e[:, :, b0:b1_].rearrange("p t b -> p b t"),
                 scalar=-1.0,
-                in1=r[:].rearrange("p t b -> p (t b)"),
+                in1=r[:, :, b0:b1_].rearrange("p t b -> p b t"),
                 op0=ALU.add,
                 op1=ALU.min,
             )
 
-        def regroup_h(i):
-            hg[i] = actp.tile([P, BS, 4], BF16, name="hg", tag="hg", align_bytes=64)
-            regroup("v", hg[i], hu[i], 0, BS)
+        def regroup_h(i, b0, b1_):
+            return
 
-        def quant_h(i):
-            hq[i] = actp.tile([P, BS], U32, name="hq", tag="hq", bufs=4, align_bytes=64)
-            hs[i] = actp.tile([P, BS], U8, name="hs", tag="hs", bufs=4, align_bytes=64)
+        def quant_h(i, b0, b1_):
+            if i not in hq:
+                hq[i] = actp.tile([P, BS], U32, name="hq", tag="hq", bufs=4, align_bytes=64)
+                hs[i] = actp.tile([P, BS], U8, name="hs", tag="hs", bufs=4, align_bytes=64)
             nc.vector.quantize_mx(
-                out=hq[i][:].bitcast(FP8X4),
-                scales=hs[i][:],
-                in_=hg[i][:].rearrange("p b t -> p (b t)"),
+                out=hq[i][:, b0:b1_].bitcast(FP8X4),
+                scales=hs[i][:, b0:b1_],
+                in_=hg[i][:, b0:b1_, :].rearrange("p b t -> p (b t)"),
             )
 
-        def mm2(g, c):
-            i = 2 * g + c
-            for h in range(2):
-                if c == 0:
-                    acc[(g, h)] = psb.tile([P, BLOCK], F32, name="acc", tag="acc", bufs=2)
-                nc.tensor.matmul_mx(
-                    out=acc[(g, h)][:],
-                    lhsT=hq[i][:, h * P : (h + 1) * P].bitcast(FP8X4),
-                    lhsT_scale=hs[i][:, h * P : (h + 1) * P],
-                    rhs=w2q[i][:].bitcast(FP8X4),
-                    rhs_scale=w2s[i][:],
-                    start=(c == 0),
-                    stop=(c == 1),
-                )
+        def mm2(i, h):
+            g, c = divmod(i, 2)
+            if c == 0:
+                acc[(g, h)] = psb.tile([P, BLOCK], F32, name="acc", tag="acc", bufs=2)
+            nc.tensor.matmul_mx(
+                out=acc[(g, h)][:],
+                lhsT=hq[i][:, h * P : (h + 1) * P].bitcast(FP8X4),
+                lhsT_scale=hs[i][:, h * P : (h + 1) * P],
+                rhs=w1q[i][:, 1, :].bitcast(FP8X4),
+                rhs_scale=w1s[i][:, 1, :],
+                start=(c == 0),
+                stop=(c == 1),
+            )
 
-        def finish(g):
-            for h in range(2):
-                res = outp.tile([P, BLOCK], F32, name="res", tag="res", bufs=4)
-                nc.vector.tensor_tensor(
-                    out=res[:], in0=acc[(g, h)][:], in1=xb[g][:, h, :], op=ALU.add
-                )
-                nc.sync.dma_start(
-                    out=out[h * P : (h + 1) * P, g * BLOCK : (g + 1) * BLOCK], in_=res[:]
-                )
+        def finish(g, h):
+            res = outp.tile([P, BLOCK], F32, name="res", tag="res", bufs=4)
+            nc.vector.tensor_tensor(out=res[:], in0=acc[(g, h)][:], in1=xb[g][:, h, :], op=ALU.add)
+            nc.sync.dma_start(out=out[h * P : (h + 1) * P, g * BLOCK : (g + 1) * BLOCK], in_=res[:])
 
-        xt0 = x_transposes(0)
+        issue_loads(-1)
+        bias_rows(0, 0, True)
+        x_transposes(0)
+        x_evac(0)
+        resid_v(0, 0)
+        resid_v(0, 1)
         b1ps = psb.tile([P, P], BF16, name="b1ps", tag="acc", bufs=2)
         nc.tensor.transpose(out=b1ps[:], in_=b1raw[:], identity=ident_b[:])
-        bias_rows(0)
-        zg0 = x_evac(0, xt0)
-        x_quant(0, zg0)
-        b1t = const.tile([P, 64], F32, name="b1t")
+        regroup_w("v", 1, 0)
+        regroup_w("s", 1, 0)
+        x_quant(0)
         nc.vector.tensor_copy(out=b1t[:], in_=b1ps[:, 0:64])
-        xt1 = x_transposes(1)
-        for eng in ("v", "s"):
-            regroup_w1(eng, 0)
-            regroup_w1(eng, 1)
-        quant_w1(0)
+        x_transposes(1)
+        bias_rows(1, 1, True)
+        regroup_w("v", 2, 0)
+        regroup_w("s", 2, 0)
+        regroup_w("v", 1, 1)
+        regroup_w("s", 1, 1)
+        quant_w(0)
         mm1(0)
-        zg1 = x_evac(1, xt1)
-        x_quant(1, zg1)
-        for eng in ("v", "s"):
-            regroup_w2(eng, 0)
-            regroup_w2(eng, 1)
-        quant_w2(0)
-        if RAW_BUFS < G:
-            load_w1(RAW_BUFS)
-            load_w2(RAW_BUFS)
+        x_evac(1)
+        regroup_w("v", 2, 1)
+        regroup_w("s", 2, 1)
+        x_quant(1)
+        issue_loads(1)
 
-        xts = {}
         for s in range(NP + 3):
             even = s % 2 == 0
             p = s - 1
-            has_p = 0 <= p < NP
             gb = s // 2
+            split = SPLIT_LAST and p == NP - 1
+            whole = 0 <= p < NP and not split
             if s + 1 < NP:
-                quant_w1(s + 1)
+                quant_w(s + 1)
                 mm1(s + 1)
-                quant_w2(s + 1)
             if not even and (s + 3) // 2 < G:
-                xts[(s + 3) // 2] = x_transposes((s + 3) // 2)
+                x_transposes((s + 3) // 2)
             if s < NP:
-                exp_relu(s)
-            if even and gb < GA:
-                resid(gb, 0)
-            if has_p:
-                elu(p)
-                regroup_h(p)
+                if SPLIT_LAST and s == NP - 1:
+                    exp_relu(s, 0, P)
+                    exp_relu(s, P, BS)
+                else:
+                    exp_relu(s, 0, BS)
+            if even and 1 <= gb + 1 < GA:
+                resid_v(gb + 1, 0)
+            if whole:
+                elu(p, 0, BS)
+                regroup_h(p, 0, BS)
             if s + 2 < NP:
-                regroup_w1("v", s + 2)
-                regroup_w2("v", s + 2)
-                regroup_w1("s", s + 2)
-                regroup_w2("s", s + 2)
-                if not even and (s + 2) // 2 + RAW_BUFS < G:
-                    load_w1((s + 2) // 2 + RAW_BUFS)
-                    load_w2((s + 2) // 2 + RAW_BUFS)
-            if not even and 0 <= (s - 3) // 2 < G:
-                finish((s - 3) // 2)
-            if has_p:
-                quant_h(p)
-                mm2(p // 2, p % 2)
-            if even and gb < GA:
-                resid(gb, 1)
-                if gb + 1 < GA:
-                    bias_rows(gb + 1)
+                regroup_w("v", 1, s + 2)
+                regroup_w("v", 2, s + 2)
+                regroup_w("s", 1, s + 2)
+                regroup_w("s", 2, s + 2)
+                issue_loads(s + 2)
+            if not even and 0 <= (s - 3) // 2 < G and not (SPLIT_LAST and (s - 3) // 2 == G - 1):
+                finish((s - 3) // 2, 0)
+                finish((s - 3) // 2, 1)
+            if whole:
+                quant_h(p, 0, BS)
+                mm2(p, 0)
+                mm2(p, 1)
+            if split:
+                elu(p, 0, P)
+                regroup_h(p, 0, P)
+                elu(p, P, BS)
+                quant_h(p, 0, P)
+                mm2(p, 0)
+                regroup_h(p, P, BS)
+                quant_h(p, P, BS)
+                mm2(p, 1)
+                finish(G - 1, 0)
+                finish(G - 1, 1)
+            if even and 1 <= gb + 1 < GA:
+                resid_v(gb + 1, 1)
+                if gb + 2 < GA:
+                    bias_rows(gb + 2, gb + 2, True)
             if GA <= gb < G:
                 resid_s(gb, s % 2)
             if GA <= (s + 1) // 2 < G:
                 resid_pe((s + 1) // 2, (s + 1) % 2)
             if even and 2 <= gb + 1 < G:
-                zg = x_evac(gb + 1, xts[gb + 1])
-                x_quant(gb + 1, zg)
+                x_evac(gb + 1)
+                x_quant(gb + 1)

@@ -22,7 +22,7 @@ FLOPS = 2 * BS * BLOCK * HID * G * 2
 
 RAW_BUFS = 6
 V1 = 0
-V2 = 512
+V2 = 464
 VHEAD = 336
 GA = 3
 SPLIT_LAST = True

@@ -12,355 +12,333 @@ ACT = mybir.ActivationFunctionType
 ALU = mybir.AluOpType
 
 P = 128
-BS = 256
-G = 8
+PACK = 4
+BATCH = 256
+BATCH_TILES = BATCH // P
+BLOCKS = 8
 BLOCK = 512
-HID = 1024
-UNIT = 512
-NP = 2 * G
-FLOPS = 2 * BS * BLOCK * HID * G * 2
+HIDDEN = 1024
+HALF = HIDDEN // 2
+PIECES = 2 * BLOCKS
+FLOPS = 2 * BATCH * BLOCK * HIDDEN * BLOCKS * 2
 
 RAW_BUFS = 6
-V1 = 0
-V2 = 464
-VHEAD = 336
-GA = 3
-SPLIT_LAST = True
+FIRST_SUMMED_BLOCK = 3
 
 
 def tile_blockresmlp_mixerblock_pb_kernel(tc, x_blocks, w1, b1, w2, b2, out):
     nc = tc.nc
     with ExitStack() as ctx:
         const = ctx.enter_context(tc.tile_pool(name="const", bufs=1))
-        rawp = ctx.enter_context(tc.tile_pool(name="rawp", bufs=RAW_BUFS))
-        grp = ctx.enter_context(tc.tile_pool(name="grp", bufs=3))
-        wq = ctx.enter_context(tc.tile_pool(name="wq", bufs=2))
-        actp = ctx.enter_context(tc.tile_pool(name="actp", bufs=2))
-        outp = ctx.enter_context(tc.tile_pool(name="outp", bufs=3))
-        psa = ctx.enter_context(tc.psum_pool(name="psa", bufs=4))
-        psb = ctx.enter_context(tc.psum_pool(name="psb", bufs=1))
+        raw_pool = ctx.enter_context(tc.tile_pool(name="raw", bufs=RAW_BUFS))
+        grouped_pool = ctx.enter_context(tc.tile_pool(name="grouped", bufs=3))
+        codes_pool = ctx.enter_context(tc.tile_pool(name="codes", bufs=5))
+        act_pool = ctx.enter_context(tc.tile_pool(name="act", bufs=2))
+        out_pool = ctx.enter_context(tc.tile_pool(name="outp", bufs=3))
+        hidden_psum = ctx.enter_context(tc.psum_pool(name="hidden_psum", bufs=4))
+        other_psum = ctx.enter_context(tc.psum_pool(name="other_psum", bufs=1))
         ctx.enter_context(tc.manual_schedule())
 
-        ident_f = const.tile([P, P], F32, name="ident_f")
-        make_identity(nc, ident_f[:])
-        ident_b = const.tile([P, P], BF16, name="ident_b")
-        make_identity(nc, ident_b[:])
-        warm_in = const.tile([P, 1], F32, name="warm_in")
-        warm_out = const.tile([P, 1], F32, name="warm_out")
-        b1raw = const.tile([P, P], BF16, name="b1raw")
-        b2z = const.tile([P, BLOCK], BF16, name="b2z")
-        b1t = const.tile([P, 64], F32, name="b1t")
-        nc.vector.memset(b2z[:], 0.0)
-        nc.vector.memset(b1raw[64:128, :], 0.0)
-        nc.vector.memset(warm_in[:], 0.0)
-        nc.scalar.activation(out=warm_out[:], in_=warm_in[:], func=ACT.Exp)
+        ident_f32 = const.tile([P, P], F32, name="ident_f32")
+        make_identity(nc, ident_f32[:])
+        ident_bf16 = const.tile([P, P], BF16, name="ident_bf16")
+        make_identity(nc, ident_bf16[:])
+        b2_rows = const.tile([P, BLOCK], BF16, name="b2_rows")
+        nc.vector.memset(b2_rows[:], 0.0)
+        b1_rows = const.tile([P, P], BF16, name="b1_rows")
+        nc.vector.memset(b1_rows[64:P, :], 0.0)
+        b1_cols = const.tile([P, PACK * PIECES], F32, name="b1_cols")
+        dummy_in = const.tile([P, 1], F32, name="dummy_in")
+        dummy_out = const.tile([P, 1], F32, name="dummy_out")
+        nc.vector.memset(dummy_in[:], 0.0)
+        nc.scalar.activation(out=dummy_out[:], in_=dummy_in[:], func=ACT.Exp)
 
         x_dram = x_blocks.rearrange("(h p) c -> p h c", p=P)
-        x_sb = [const.tile([P, 2, BLOCK], BF16, name="x_sb%d" % g) for g in range(G)]
-        raw1 = {}
-        raw2 = {}
+        x_sb = [const.tile([P, BATCH_TILES, BLOCK], BF16, name="x_sb%d" % g) for g in range(BLOCKS)]
+        raw_w1 = {}
+        raw_w2 = {}
 
         def load(kind, i):
             g, c = divmod(i, 2)
             if kind == "b1":
                 nc.sync.dma_start(
-                    out=b1raw[0:64, :], in_=b1.rearrange("g o (m p) -> (g o m) p", p=P)
+                    out=b1_rows[0:64, :], in_=b1.rearrange("g o (m p) -> (g o m) p", p=P)
                 )
             elif kind == "b2":
-                nc.sync.dma_start(out=b2z[0:G, :], in_=b2.rearrange("g o d -> (g o) d"))
+                nc.sync.dma_start(out=b2_rows[0:BLOCKS, :], in_=b2.rearrange("g o d -> (g o) d"))
             elif kind == "x":
                 nc.sync.dma_start(out=x_sb[i][:], in_=x_dram[:, :, i * BLOCK : (i + 1) * BLOCK])
             elif kind == "w1":
-                raw1[i] = rawp.tile([P, 4, UNIT], BF16, name="raw1", tag="raw1")
+                raw_w1[i] = raw_pool.tile([P, PACK, HALF], BF16, name="raw_w1", tag="raw_w1")
                 for u in range(2):
                     nc.sync.dma_start(
-                        out=raw1[i][:, 2 * u : 2 * u + 2, :],
-                        in_=w1[g][256 * u : 256 * (u + 1), c * UNIT : (c + 1) * UNIT].rearrange(
+                        out=raw_w1[i][:, 2 * u : 2 * u + 2, :],
+                        in_=w1[g][256 * u : 256 * (u + 1), c * HALF : (c + 1) * HALF].rearrange(
                             "(q e) n -> q e n", e=2
                         ),
                     )
             else:
-                raw2[i] = rawp.tile([P, 4, UNIT], BF16, name="raw2", tag="raw2")
+                raw_w2[i] = raw_pool.tile([P, PACK, BLOCK], BF16, name="raw_w2", tag="raw_w2")
                 nc.sync.dma_start(
-                    out=raw2[i][:],
-                    in_=w2[g][c * UNIT : (c + 1) * UNIT, :].rearrange("(t p) d -> p t d", p=P),
+                    out=raw_w2[i][:],
+                    in_=w2[g][c * HALF : (c + 1) * HALF, :].rearrange("(t p) d -> p t d", p=P),
                 )
 
-        order = [("b1", 0), ("b2", 0), ("x", 0), ("w1", 0), ("w2", 0), ("w1", 1), ("x", 1), ("w2", 1)]
-        for i in range(2, NP):
-            order.append(("w1", i))
-            order.append(("w2", i))
-            if i % 2 == 0 and i // 2 + 1 < G:
-                order.append(("x", i // 2 + 1))
-        issued = [0]
+        load_order = [("b1", 0), ("b2", 0), ("x", 0), ("w1", 0), ("w2", 0), ("w1", 1), ("x", 1), ("w2", 1)]
+        for i in range(2, PIECES):
+            load_order.append(("w1", i))
+            load_order.append(("w2", i))
+            if i % 2 == 0 and i // 2 + 1 < BLOCKS:
+                load_order.append(("x", i // 2 + 1))
+        loads_started = [0]
 
-        def issue_loads(done):
-            while issued[0] < len(order):
-                kind, i = order[issued[0]]
-                if kind in ("w1", "w2") and i - RAW_BUFS > done:
+        def start_loads(regrouped):
+            while loads_started[0] < len(load_order):
+                kind, i = load_order[loads_started[0]]
+                if kind in ("w1", "w2") and i - RAW_BUFS > regrouped:
                     break
                 load(kind, i)
-                issued[0] += 1
+                loads_started[0] += 1
 
-        xts = {}
-        zgs = {}
-        zq = {}
-        zs = {}
-        bbs = {}
-        xb = {}
-        g1 = {}
-        g2 = {}
-        w1q = {}
-        w1s = {}
-        w2q = {}
-        w2s = {}
-        hp = {}
-        er = {}
-        hu = {}
-        hg = {}
-        hq = {}
-        hs = {}
-        acc = {}
+        x_psum = {}
+        z_grouped = {}
+        z_codes = {}
+        z_scales = {}
+        b2_psum = {}
+        resid = {}
+        w_grouped = {}
+        w_codes = {}
+        w_scales = {}
+        h_psum = {}
+        exp_and_relu = {}
+        h_grouped = {}
+        h_codes = {}
+        h_scales = {}
+        out_psum = {}
 
-        def x_transposes(g):
-            xts[g] = psb.tile([P, 2, BS], F32, name="xt", tag="xt")
+        def transpose_x(g):
+            x_psum[g] = other_psum.tile([P, 2, BATCH], F32, name="x_psum", tag="x_psum")
             words = x_sb[g][:].rearrange("p h c -> p (h c)").bitcast(F32)
             for u in range(2):
-                for h in range(2):
-                    w0 = h * 256 + 128 * u
+                for h in range(BATCH_TILES):
+                    first = h * (BLOCK // 2) + P * u
                     nc.tensor.transpose(
-                        out=xts[g][:, u, h * P : (h + 1) * P],
-                        in_=words[:, w0 : w0 + P],
-                        identity=ident_f[:],
+                        out=x_psum[g][:, u, h * P : (h + 1) * P],
+                        in_=words[:, first : first + P],
+                        identity=ident_f32[:],
                     )
 
-        def x_evac(g):
-            zgs[g] = actp.tile([P, 4 * BS], BF16, name="zg", tag="zg", align_bytes=64)
+        def copy_x(g):
+            z_grouped[g] = act_pool.tile(
+                [P, PACK * BATCH], BF16, name="z_grouped", tag="z_grouped", align_bytes=64
+            )
             nc.scalar.copy(
-                out=zgs[g][:].bitcast(F32).rearrange("p (b u) -> p b u", u=2),
-                in_=xts[g][:].rearrange("p u b -> p b u"),
+                out=z_grouped[g][:].bitcast(F32).rearrange("p (b u) -> p b u", u=2),
+                in_=x_psum[g][:].rearrange("p u b -> p b u"),
             )
 
-        def x_quant(g):
-            zq[g] = actp.tile([P, BS], U32, name="zq", tag="zq", bufs=3, align_bytes=64)
-            zs[g] = actp.tile([P, BS], U8, name="zs", tag="zs", bufs=3, align_bytes=64)
-            nc.vector.quantize_mx(out=zq[g][:].bitcast(FP8X4), scales=zs[g][:], in_=zgs[g][:])
+        def quantise_x(g):
+            z_codes[g] = act_pool.tile([P, BATCH], U32, name="z_codes", tag="z_codes", bufs=3, align_bytes=64)
+            z_scales[g] = act_pool.tile([P, BATCH], U8, name="z_scales", tag="z_scales", bufs=3, align_bytes=64)
+            nc.vector.quantize_mx(
+                out=z_codes[g][:].bitcast(FP8X4), scales=z_scales[g][:], in_=z_grouped[g][:]
+            )
 
-        def bias_rows(key, g, stop):
-            bbs[key] = psb.tile([P, BLOCK], F32, name="bb", tag="bb")
+        def spread_b2(key, g, stop):
+            b2_psum[key] = other_psum.tile([P, BLOCK], F32, name="b2_psum", tag="b2_psum")
             nc.tensor.matmul(
-                out=bbs[key][:],
-                lhsT=ident_b[:, g : g + 1].to_broadcast([P, P]),
-                rhs=b2z[:],
+                out=b2_psum[key][:],
+                lhsT=ident_bf16[:, g : g + 1].to_broadcast([P, P]),
+                rhs=b2_rows[:],
                 start=True,
                 stop=stop,
             )
 
         def resid_tile(g):
-            if g not in xb:
-                xb[g] = outp.tile([P, 2, BLOCK], F32, name="xb", tag="xb")
-            return xb[g]
+            if g not in resid:
+                resid[g] = out_pool.tile([P, BATCH_TILES, BLOCK], F32, name="resid", tag="resid")
+            return resid[g]
 
-        def resid_v(g, h):
+        def add_x_b2(g, h):
             nc.vector.tensor_tensor(
-                out=resid_tile(g)[:, h, :], in0=bbs[g][:], in1=x_sb[g][:, h, :], op=ALU.add
+                out=resid_tile(g)[:, h, :], in0=b2_psum[g][:], in1=x_sb[g][:, h, :], op=ALU.add
             )
 
-        def resid_pe(g, h):
-            bias_rows((g, h), g, False)
+        def sum_x_b2(g, h):
+            spread_b2((g, h), g, False)
             nc.tensor.matmul(
-                out=bbs[(g, h)][:], lhsT=ident_b[:], rhs=x_sb[g][:, h, :], start=False, stop=True
+                out=b2_psum[(g, h)][:], lhsT=ident_bf16[:], rhs=x_sb[g][:, h, :], start=False, stop=True
             )
 
-        def resid_s(g, h):
-            nc.scalar.copy(out=resid_tile(g)[:, h, :], in_=bbs[(g, h)][:])
+        def copy_x_b2(g, h):
+            nc.scalar.copy(out=resid_tile(g)[:, h, :], in_=b2_psum[(g, h)][:])
 
-        def regroup(eng, dst, src, c0, c1):
-            if c1 <= c0:
-                return
-            o = dst[:, c0:c1, :].rearrange("p (c i) t -> p c t i", i=4)
-            s = src[:, :, c0:c1].rearrange("p t (c i) -> p c t i", i=4)
-            if eng == "v":
-                nc.vector.tensor_copy(out=o, in_=s)
-            else:
-                nc.scalar.copy(out=o, in_=s)
+        def regroup(copy, i, kind, raw):
+            if i not in w_grouped:
+                w_grouped[i] = grouped_pool.tile(
+                    [P, 2, HALF, PACK], BF16, name="w_grouped", tag="w_grouped", align_bytes=64
+                )
+            copy(
+                out=w_grouped[i][:, kind, :, :].rearrange("p (c i) t -> p c t i", i=4),
+                in_=raw[:].rearrange("p t (c i) -> p c t i", i=4),
+            )
 
-        def regroup_w(eng, kind, i):
-            if i not in g1:
-                g1[i] = grp.tile([P, 2, UNIT, 4], BF16, name="gw", tag="gw", align_bytes=64)
-            raws, share = (raw1, V1) if kind == 1 else (raw2, V2)
-            v = VHEAD if i < 2 else share
-            c0, c1 = (0, v) if eng == "v" else (v, UNIT)
-            regroup(eng, g1[i][:, kind - 1, :, :], raws[i], c0, c1)
+        def regroup_w1(i):
+            regroup(nc.scalar.copy, i, 0, raw_w1[i])
 
-        def quant_w(i):
-            w1q[i] = wq.tile([P, 2, UNIT], U32, name="wc", tag="wc", bufs=5, align_bytes=64)
-            w1s[i] = wq.tile([P, 2, UNIT], U8, name="ws", tag="ws", bufs=5, align_bytes=64)
+        def regroup_w2(i):
+            regroup(nc.vector.tensor_copy, i, 1, raw_w2[i])
+
+        def quantise_w(i):
+            w_codes[i] = codes_pool.tile([P, 2, HALF], U32, name="w_codes", tag="w_codes", align_bytes=64)
+            w_scales[i] = codes_pool.tile([P, 2, HALF], U8, name="w_scales", tag="w_scales", align_bytes=64)
             nc.vector.quantize_mx(
-                out=w1q[i][:].rearrange("p k n -> p (k n)").bitcast(FP8X4),
-                scales=w1s[i][:].rearrange("p k n -> p (k n)"),
-                in_=g1[i][:].rearrange("p k n t -> p (k n t)"),
+                out=w_codes[i][:].rearrange("p k n -> p (k n)").bitcast(FP8X4),
+                scales=w_scales[i][:].rearrange("p k n -> p (k n)"),
+                in_=w_grouped[i][:].rearrange("p k n t -> p (k n t)"),
             )
 
-        def mm1(i):
-            g = i // 2
-            hp[i] = [
-                psa.tile([P, 2, BS], F32, name="hp0", tag="a"),
-                psa.tile([P, 2, BS], F32, name="hp1", tag="a"),
+        def first_matmul(i):
+            h_psum[i] = [
+                hidden_psum.tile([P, 2, BATCH], F32, name="h_psum%d" % k, tag="h_psum") for k in range(2)
             ]
-            for t in range(4):
+            for t in range(PACK):
                 nc.tensor.matmul_mx(
-                    out=hp[i][t // 2][:, t % 2, :],
-                    lhsT=w1q[i][:, 0, t * P : (t + 1) * P].bitcast(FP8X4),
-                    lhsT_scale=w1s[i][:, 0, t * P : (t + 1) * P],
-                    rhs=zq[g][:].bitcast(FP8X4),
-                    rhs_scale=zs[g][:],
+                    out=h_psum[i][t // 2][:, t % 2, :],
+                    lhsT=w_codes[i][:, 0, t * P : (t + 1) * P].bitcast(FP8X4),
+                    lhsT_scale=w_scales[i][:, 0, t * P : (t + 1) * P],
+                    rhs=z_codes[i // 2][:].bitcast(FP8X4),
+                    rhs_scale=z_scales[i // 2][:],
                     start=True,
                     stop=True,
                 )
 
-        def exp_relu(i, b0, b1_):
-            if i not in er:
-                er[i] = (
-                    actp.tile([P, 4, BS], F32, name="e", tag="e", bufs=3),
-                    actp.tile([P, 4, BS], F32, name="r", tag="r", bufs=3),
-                )
-            for t in range(4):
-                col = 4 * i + t
-                for dst, func in zip(er[i], (ACT.Exp, ACT.Relu)):
+        def parts(i):
+            return ((0,), (1,)) if i == PIECES - 1 else ((0, 1),)
+
+        def rows(part):
+            return slice(part[0] * P, (part[-1] + 1) * P)
+
+        def exp_relu(i, part):
+            if i not in exp_and_relu:
+                exp_and_relu[i] = [
+                    act_pool.tile([P, PACK, BATCH], F32, name=name, tag=name, bufs=3) for name in ("e", "r")
+                ]
+            for t in range(PACK):
+                for dst, func in zip(exp_and_relu[i], (ACT.Exp, ACT.Relu)):
                     nc.scalar.activation(
-                        out=dst[:, t, b0:b1_],
-                        in_=hp[i][t // 2][:, t % 2, b0:b1_],
+                        out=dst[:, t, rows(part)],
+                        in_=h_psum[i][t // 2][:, t % 2, rows(part)],
                         func=func,
-                        bias=b1t[:, col : col + 1],
+                        bias=b1_cols[:, PACK * i + t : PACK * i + t + 1],
                         scale=1.0,
                     )
 
-        def elu(i, b0, b1_):
-            e, r = er[i]
-            if i not in hg:
-                hg[i] = actp.tile([P, BS, 4], BF16, name="hg", tag="hg", align_bytes=64)
+        def elu(i, part):
+            e, r = exp_and_relu[i]
+            if i not in h_grouped:
+                h_grouped[i] = act_pool.tile(
+                    [P, BATCH, PACK], BF16, name="h_grouped", tag="h_grouped", align_bytes=64
+                )
             nc.vector.scalar_tensor_tensor(
-                out=hg[i][:, b0:b1_, :],
-                in0=e[:, :, b0:b1_].rearrange("p t b -> p b t"),
+                out=h_grouped[i][:, rows(part), :],
+                in0=e[:, :, rows(part)].rearrange("p t b -> p b t"),
                 scalar=-1.0,
-                in1=r[:, :, b0:b1_].rearrange("p t b -> p b t"),
+                in1=r[:, :, rows(part)].rearrange("p t b -> p b t"),
                 op0=ALU.add,
                 op1=ALU.min,
             )
 
-        def regroup_h(i, b0, b1_):
-            return
-
-        def quant_h(i, b0, b1_):
-            if i not in hq:
-                hq[i] = actp.tile([P, BS], U32, name="hq", tag="hq", bufs=4, align_bytes=64)
-                hs[i] = actp.tile([P, BS], U8, name="hs", tag="hs", bufs=4, align_bytes=64)
+        def quantise_h(i, part):
+            if i not in h_codes:
+                h_codes[i] = act_pool.tile([P, BATCH], U32, name="h_codes", tag="h_codes", bufs=4, align_bytes=64)
+                h_scales[i] = act_pool.tile([P, BATCH], U8, name="h_scales", tag="h_scales", bufs=4, align_bytes=64)
             nc.vector.quantize_mx(
-                out=hq[i][:, b0:b1_].bitcast(FP8X4),
-                scales=hs[i][:, b0:b1_],
-                in_=hg[i][:, b0:b1_, :].rearrange("p b t -> p (b t)"),
+                out=h_codes[i][:, rows(part)].bitcast(FP8X4),
+                scales=h_scales[i][:, rows(part)],
+                in_=h_grouped[i][:, rows(part), :].rearrange("p b t -> p (b t)"),
             )
 
-        def mm2(i, h):
+        def second_matmul(i, h):
             g, c = divmod(i, 2)
             if c == 0:
-                acc[(g, h)] = psb.tile([P, BLOCK], F32, name="acc", tag="acc", bufs=2)
+                out_psum[(g, h)] = other_psum.tile([P, BLOCK], F32, name="out_psum", tag="out_psum", bufs=2)
             nc.tensor.matmul_mx(
-                out=acc[(g, h)][:],
-                lhsT=hq[i][:, h * P : (h + 1) * P].bitcast(FP8X4),
-                lhsT_scale=hs[i][:, h * P : (h + 1) * P],
-                rhs=w1q[i][:, 1, :].bitcast(FP8X4),
-                rhs_scale=w1s[i][:, 1, :],
+                out=out_psum[(g, h)][:],
+                lhsT=h_codes[i][:, h * P : (h + 1) * P].bitcast(FP8X4),
+                lhsT_scale=h_scales[i][:, h * P : (h + 1) * P],
+                rhs=w_codes[i][:, 1, :].bitcast(FP8X4),
+                rhs_scale=w_scales[i][:, 1, :],
                 start=(c == 0),
                 stop=(c == 1),
             )
 
         def finish(g, h):
-            res = outp.tile([P, BLOCK], F32, name="res", tag="res", bufs=4)
-            nc.vector.tensor_tensor(out=res[:], in0=acc[(g, h)][:], in1=xb[g][:, h, :], op=ALU.add)
-            nc.sync.dma_start(out=out[h * P : (h + 1) * P, g * BLOCK : (g + 1) * BLOCK], in_=res[:])
+            result = out_pool.tile([P, BLOCK], F32, name="result", tag="result", bufs=4)
+            nc.vector.tensor_tensor(
+                out=result[:], in0=out_psum[(g, h)][:], in1=resid[g][:, h, :], op=ALU.add
+            )
+            nc.sync.dma_start(out=out[h * P : (h + 1) * P, g * BLOCK : (g + 1) * BLOCK], in_=result[:])
 
-        issue_loads(-1)
-        bias_rows(0, 0, True)
-        x_transposes(0)
-        x_evac(0)
-        resid_v(0, 0)
-        resid_v(0, 1)
-        b1ps = psb.tile([P, P], BF16, name="b1ps", tag="acc", bufs=2)
-        nc.tensor.transpose(out=b1ps[:], in_=b1raw[:], identity=ident_b[:])
-        regroup_w("v", 1, 0)
-        regroup_w("s", 1, 0)
-        x_quant(0)
-        nc.vector.tensor_copy(out=b1t[:], in_=b1ps[:, 0:64])
-        x_transposes(1)
-        bias_rows(1, 1, True)
-        regroup_w("v", 2, 0)
-        regroup_w("s", 2, 0)
-        regroup_w("v", 1, 1)
-        regroup_w("s", 1, 1)
-        quant_w(0)
-        mm1(0)
-        x_evac(1)
-        regroup_w("v", 2, 1)
-        regroup_w("s", 2, 1)
-        x_quant(1)
-        issue_loads(1)
+        start_loads(-1)
+        spread_b2(0, 0, True)
+        transpose_x(0)
+        copy_x(0)
+        for h in range(BATCH_TILES):
+            add_x_b2(0, h)
+        b1_psum = other_psum.tile([P, P], BF16, name="b1_psum", tag="out_psum", bufs=2)
+        nc.tensor.transpose(out=b1_psum[:], in_=b1_rows[:], identity=ident_bf16[:])
+        regroup_w1(0)
+        quantise_x(0)
+        nc.vector.tensor_copy(out=b1_cols[:], in_=b1_psum[:, 0 : PACK * PIECES])
+        transpose_x(1)
+        spread_b2(1, 1, True)
+        regroup_w2(0)
+        regroup_w1(1)
+        quantise_w(0)
+        first_matmul(0)
+        copy_x(1)
+        regroup_w2(1)
+        quantise_x(1)
+        start_loads(1)
 
-        for s in range(NP + 3):
+        for s in range(PIECES + 2):
             even = s % 2 == 0
-            p = s - 1
-            gb = s // 2
-            split = SPLIT_LAST and p == NP - 1
-            whole = 0 <= p < NP and not split
-            if s + 1 < NP:
-                quant_w(s + 1)
-                mm1(s + 1)
-            if not even and (s + 3) // 2 < G:
-                x_transposes((s + 3) // 2)
-            if s < NP:
-                if SPLIT_LAST and s == NP - 1:
-                    exp_relu(s, 0, P)
-                    exp_relu(s, P, BS)
-                else:
-                    exp_relu(s, 0, BS)
-            if even and 1 <= gb + 1 < GA:
-                resid_v(gb + 1, 0)
-            if whole:
-                elu(p, 0, BS)
-                regroup_h(p, 0, BS)
-            if s + 2 < NP:
-                regroup_w("v", 1, s + 2)
-                regroup_w("v", 2, s + 2)
-                regroup_w("s", 1, s + 2)
-                regroup_w("s", 2, s + 2)
-                issue_loads(s + 2)
-            if not even and 0 <= (s - 3) // 2 < G and not (SPLIT_LAST and (s - 3) // 2 == G - 1):
-                finish((s - 3) // 2, 0)
-                finish((s - 3) // 2, 1)
-            if whole:
-                quant_h(p, 0, BS)
-                mm2(p, 0)
-                mm2(p, 1)
-            if split:
-                elu(p, 0, P)
-                regroup_h(p, 0, P)
-                elu(p, P, BS)
-                quant_h(p, 0, P)
-                mm2(p, 0)
-                regroup_h(p, P, BS)
-                quant_h(p, P, BS)
-                mm2(p, 1)
-                finish(G - 1, 0)
-                finish(G - 1, 1)
-            if even and 1 <= gb + 1 < GA:
-                resid_v(gb + 1, 1)
-                if gb + 2 < GA:
-                    bias_rows(gb + 2, gb + 2, True)
-            if GA <= gb < G:
-                resid_s(gb, s % 2)
-            if GA <= (s + 1) // 2 < G:
-                resid_pe((s + 1) // 2, (s + 1) % 2)
-            if even and 2 <= gb + 1 < G:
-                x_evac(gb + 1)
-                x_quant(gb + 1)
+            g = s // 2
+            behind = s - 1
+            if s + 1 < PIECES:
+                quantise_w(s + 1)
+                first_matmul(s + 1)
+            if not even and (s + 3) // 2 < BLOCKS:
+                transpose_x((s + 3) // 2)
+            if s < PIECES:
+                for part in parts(s):
+                    exp_relu(s, part)
+            if even and g + 1 < FIRST_SUMMED_BLOCK:
+                add_x_b2(g + 1, 0)
+            if 0 <= behind < PIECES:
+                for part in parts(behind):
+                    elu(behind, part)
+            if s + 2 < PIECES:
+                regroup_w2(s + 2)
+                regroup_w1(s + 2)
+                start_loads(s + 2)
+            if FIRST_SUMMED_BLOCK <= behind // 2 < BLOCKS:
+                copy_x_b2(behind // 2, behind % 2)
+            if not even and s >= 3:
+                for h in range(BATCH_TILES):
+                    finish((s - 3) // 2, h)
+            if 0 <= behind < PIECES:
+                for part in parts(behind):
+                    quantise_h(behind, part)
+                    for h in part:
+                        second_matmul(behind, h)
+            if even and g + 1 < FIRST_SUMMED_BLOCK:
+                add_x_b2(g + 1, 1)
+                if g + 2 < FIRST_SUMMED_BLOCK:
+                    spread_b2(g + 2, g + 2, True)
+            if FIRST_SUMMED_BLOCK <= g < BLOCKS:
+                sum_x_b2(g, s % 2)
+            if even and 2 <= g + 1 < BLOCKS:
+                copy_x(g + 1)
+                quantise_x(g + 1)

@@ -222,10 +222,11 @@ def tile_blockresmlp_mixerblock_pb_kernel(tc, x_blocks, w1, b1, w2, b2, out):
         def exp_relu(i, part):
             if i not in exp_and_relu:
                 exp_and_relu[i] = [
-                    act_pool.tile([P, PACK, BATCH], F32, name=name, tag=name, bufs=3) for name in ("e", "r")
+                    act_pool.tile([P, PACK, BATCH], dtype, name=name, tag=name, bufs=3)
+                    for name, dtype in (("e", F32), ("r", BF16))
                 ]
-            for t in range(PACK):
-                for dst, func in zip(exp_and_relu[i], (ACT.Exp, ACT.Relu)):
+            for dst, func in zip(exp_and_relu[i], (ACT.Exp, ACT.Relu)):
+                for t in range(PACK):
                     nc.scalar.activation(
                         out=dst[:, t, rows(part)],
                         in_=h_psum[i][t // 2][:, t % 2, rows(part)],

@@ -23,6 +23,8 @@ PIECES = 2 * BLOCKS
 FLOPS = 2 * BATCH * BLOCK * HIDDEN * BLOCKS * 2
 
 RAW_BUFS = 6
+VECTOR_W1 = 64
+SCALAR_W1 = HALF - VECTOR_W1
 FIRST_SUMMED_BLOCK = 3
 
 
@@ -55,8 +57,12 @@ def tile_blockresmlp_mixerblock_pb_kernel(tc, x_blocks, w1, b1, w2, b2, out):
 
         x_dram = x_blocks.rearrange("(h p) c -> p h c", p=P)
         x_sb = [const.tile([P, BATCH_TILES, BLOCK], BF16, name="x_sb%d" % g) for g in range(BLOCKS)]
-        raw_w1 = {}
-        raw_w2 = {}
+        raw = {}
+
+        def raw_tile(i):
+            if i not in raw:
+                raw[i] = raw_pool.tile([P, PACK, 2 * HALF], BF16, name="raw", tag="raw")
+            return raw[i]
 
         def load(kind, i):
             g, c = divmod(i, 2)
@@ -69,18 +75,16 @@ def tile_blockresmlp_mixerblock_pb_kernel(tc, x_blocks, w1, b1, w2, b2, out):
             elif kind == "x":
                 nc.sync.dma_start(out=x_sb[i][:], in_=x_dram[:, :, i * BLOCK : (i + 1) * BLOCK])
             elif kind == "w1":
-                raw_w1[i] = raw_pool.tile([P, PACK, HALF], BF16, name="raw_w1", tag="raw_w1")
                 for u in range(2):
                     nc.sync.dma_start(
-                        out=raw_w1[i][:, 2 * u : 2 * u + 2, :],
+                        out=raw_tile(i)[:, 2 * u : 2 * u + 2, 0:HALF],
                         in_=w1[g][256 * u : 256 * (u + 1), c * HALF : (c + 1) * HALF].rearrange(
                             "(q e) n -> q e n", e=2
                         ),
                     )
             else:
-                raw_w2[i] = raw_pool.tile([P, PACK, BLOCK], BF16, name="raw_w2", tag="raw_w2")
                 nc.sync.dma_start(
-                    out=raw_w2[i][:],
+                    out=raw_tile(i)[:, :, HALF : 2 * HALF],
                     in_=w2[g][c * HALF : (c + 1) * HALF, :].rearrange("(t p) d -> p t d", p=P),
                 )
 
@@ -173,21 +177,21 @@ def tile_blockresmlp_mixerblock_pb_kernel(tc, x_blocks, w1, b1, w2, b2, out):
         def copy_x_b2(g, h):
             nc.scalar.copy(out=resid_tile(g)[:, h, :], in_=b2_psum[(g, h)][:])
 
-        def regroup(copy, i, kind, raw):
+        def regroup(copy, i, first, last):
             if i not in w_grouped:
                 w_grouped[i] = grouped_pool.tile(
-                    [P, 2, HALF, PACK], BF16, name="w_grouped", tag="w_grouped", align_bytes=64
+                    [P, 2 * HALF, PACK], BF16, name="w_grouped", tag="w_grouped", align_bytes=64
                 )
             copy(
-                out=w_grouped[i][:, kind, :, :].rearrange("p (c i) t -> p c t i", i=4),
-                in_=raw[:].rearrange("p t (c i) -> p c t i", i=4),
+                out=w_grouped[i][:, first:last, :].rearrange("p (c i) t -> p c t i", i=4),
+                in_=raw[i][:, :, first:last].rearrange("p t (c i) -> p c t i", i=4),
             )
 
-        def regroup_w1(i):
-            regroup(nc.scalar.copy, i, 0, raw_w1[i])
+        def regroup_scalar(i):
+            regroup(nc.scalar.copy, i, 0, SCALAR_W1)
 
-        def regroup_w2(i):
-            regroup(nc.vector.tensor_copy, i, 1, raw_w2[i])
+        def regroup_vector(i):
+            regroup(nc.vector.tensor_copy, i, SCALAR_W1, 2 * HALF)
 
         def quantise_w(i):
             w_codes[i] = codes_pool.tile([P, 2, HALF], U32, name="w_codes", tag="w_codes", align_bytes=64)
@@ -195,7 +199,7 @@ def tile_blockresmlp_mixerblock_pb_kernel(tc, x_blocks, w1, b1, w2, b2, out):
             nc.vector.quantize_mx(
                 out=w_codes[i][:].rearrange("p k n -> p (k n)").bitcast(FP8X4),
                 scales=w_scales[i][:].rearrange("p k n -> p (k n)"),
-                in_=w_grouped[i][:].rearrange("p k n t -> p (k n t)"),
+                in_=w_grouped[i][:].rearrange("p n t -> p (n t)"),
             )
 
         def first_matmul(i):
@@ -289,17 +293,17 @@ def tile_blockresmlp_mixerblock_pb_kernel(tc, x_blocks, w1, b1, w2, b2, out):
             add_x_b2(0, h)
         b1_psum = other_psum.tile([P, P], BF16, name="b1_psum", tag="out_psum", bufs=2)
         nc.tensor.transpose(out=b1_psum[:], in_=b1_rows[:], identity=ident_bf16[:])
-        regroup_w1(0)
+        regroup_scalar(0)
         quantise_x(0)
         nc.vector.tensor_copy(out=b1_cols[:], in_=b1_psum[:, 0 : PACK * PIECES])
         transpose_x(1)
         spread_b2(1, 1, True)
-        regroup_w2(0)
-        regroup_w1(1)
+        regroup_vector(0)
+        regroup_scalar(1)
         quantise_w(0)
         first_matmul(0)
         copy_x(1)
-        regroup_w2(1)
+        regroup_vector(1)
         quantise_x(1)
         start_loads(1)
 
@@ -321,8 +325,8 @@ def tile_blockresmlp_mixerblock_pb_kernel(tc, x_blocks, w1, b1, w2, b2, out):
                 for part in parts(behind):
                     elu(behind, part)
             if s + 2 < PIECES:
-                regroup_w2(s + 2)
-                regroup_w1(s + 2)
+                regroup_vector(s + 2)
+                regroup_scalar(s + 2)
                 start_loads(s + 2)
             if FIRST_SUMMED_BLOCK <= behind // 2 < BLOCKS:
                 copy_x_b2(behind // 2, behind % 2)

@@ -23,8 +23,10 @@ PIECES = 2 * BLOCKS
 FLOPS = 2 * BATCH * BLOCK * HIDDEN * BLOCKS * 2
 
 RAW_BUFS = 6
-VECTOR_W1 = 64
+VECTOR_W1 = 16
 SCALAR_W1 = HALF - VECTOR_W1
+HEAD_PIECES = 2
+FIRST_HALF = HALF // 2
 FIRST_SUMMED_BLOCK = 3
 
 
@@ -58,11 +60,17 @@ def tile_blockresmlp_mixerblock_pb_kernel(tc, x_blocks, w1, b1, w2, b2, out):
         x_dram = x_blocks.rearrange("(h p) c -> p h c", p=P)
         x_sb = [const.tile([P, BATCH_TILES, BLOCK], BF16, name="x_sb%d" % g) for g in range(BLOCKS)]
         raw = {}
+        head_raw = {}
 
-        def raw_tile(i):
+        def raw_columns(i, first, last):
+            if i < HEAD_PIECES:
+                key = (i, first, last)
+                if key not in head_raw:
+                    head_raw[key] = const.tile([P, PACK, last - first], BF16, name="raw_%d_%d_%d" % key)
+                return head_raw[key][:]
             if i not in raw:
                 raw[i] = raw_pool.tile([P, PACK, 2 * HALF], BF16, name="raw", tag="raw")
-            return raw[i]
+            return raw[i][:, :, first:last]
 
         def load(kind, i):
             g, c = divmod(i, 2)
@@ -75,20 +83,21 @@ def tile_blockresmlp_mixerblock_pb_kernel(tc, x_blocks, w1, b1, w2, b2, out):
             elif kind == "x":
                 nc.sync.dma_start(out=x_sb[i][:], in_=x_dram[:, :, i * BLOCK : (i + 1) * BLOCK])
             elif kind == "w1":
-                for u in range(2):
-                    nc.sync.dma_start(
-                        out=raw_tile(i)[:, 2 * u : 2 * u + 2, 0:HALF],
-                        in_=w1[g][256 * u : 256 * (u + 1), c * HALF : (c + 1) * HALF].rearrange(
-                            "(q e) n -> q e n", e=2
-                        ),
-                    )
+                for first, last in ((0, FIRST_HALF), (FIRST_HALF, HALF)) if i == 0 else ((0, HALF),):
+                    for u in range(2):
+                        nc.sync.dma_start(
+                            out=raw_columns(i, first, last)[:, 2 * u : 2 * u + 2, :],
+                            in_=w1[g][
+                                256 * u : 256 * (u + 1), c * HALF + first : c * HALF + last
+                            ].rearrange("(q e) n -> q e n", e=2),
+                        )
             else:
                 nc.sync.dma_start(
-                    out=raw_tile(i)[:, :, HALF : 2 * HALF],
+                    out=raw_columns(i, HALF, 2 * HALF),
                     in_=w2[g][c * HALF : (c + 1) * HALF, :].rearrange("(t p) d -> p t d", p=P),
                 )
 
-        load_order = [("b1", 0), ("b2", 0), ("x", 0), ("w1", 0), ("w2", 0), ("w1", 1), ("x", 1), ("w2", 1)]
+        load_order = [("w1", 0), ("b2", 0), ("x", 0), ("b1", 0), ("w1", 1), ("w2", 0), ("w2", 1), ("x", 1)]
         for i in range(2, PIECES):
             load_order.append(("w1", i))
             load_order.append(("w2", i))
@@ -99,7 +108,7 @@ def tile_blockresmlp_mixerblock_pb_kernel(tc, x_blocks, w1, b1, w2, b2, out):
         def start_loads(regrouped):
             while loads_started[0] < len(load_order):
                 kind, i = load_order[loads_started[0]]
-                if kind in ("w1", "w2") and i - RAW_BUFS > regrouped:
+                if kind in ("w1", "w2") and i - RAW_BUFS >= HEAD_PIECES and i - RAW_BUFS > regrouped:
                     break
                 load(kind, i)
                 loads_started[0] += 1
@@ -184,22 +193,24 @@ def tile_blockresmlp_mixerblock_pb_kernel(tc, x_blocks, w1, b1, w2, b2, out):
                 )
             copy(
                 out=w_grouped[i][:, first:last, :].rearrange("p (c i) t -> p c t i", i=4),
-                in_=raw[i][:, :, first:last].rearrange("p t (c i) -> p c t i", i=4),
+                in_=raw_columns(i, first, last).rearrange("p t (c i) -> p c t i", i=4),
             )
 
         def regroup_scalar(i):
-            regroup(nc.scalar.copy, i, 0, SCALAR_W1)
+            regroup(nc.scalar.copy, i, 0, SCALAR_W1 if i >= HEAD_PIECES else HALF)
 
         def regroup_vector(i):
-            regroup(nc.vector.tensor_copy, i, SCALAR_W1, 2 * HALF)
+            regroup(nc.vector.tensor_copy, i, SCALAR_W1 if i >= HEAD_PIECES else HALF, 2 * HALF)
 
-        def quantise_w(i):
-            w_codes[i] = codes_pool.tile([P, 2, HALF], U32, name="w_codes", tag="w_codes", align_bytes=64)
-            w_scales[i] = codes_pool.tile([P, 2, HALF], U8, name="w_scales", tag="w_scales", align_bytes=64)
+        def quantise_w(i, kinds=2, first=0):
+            if i not in w_codes:
+                w_codes[i] = codes_pool.tile([P, 2, HALF], U32, name="w_codes", tag="w_codes", align_bytes=64)
+                w_scales[i] = codes_pool.tile([P, 2, HALF], U8, name="w_scales", tag="w_scales", align_bytes=64)
+            last = first + kinds
             nc.vector.quantize_mx(
-                out=w_codes[i][:].rearrange("p k n -> p (k n)").bitcast(FP8X4),
-                scales=w_scales[i][:].rearrange("p k n -> p (k n)"),
-                in_=w_grouped[i][:].rearrange("p n t -> p (n t)"),
+                out=w_codes[i][:, first:last, :].rearrange("p k n -> p (k n)").bitcast(FP8X4),
+                scales=w_scales[i][:, first:last, :].rearrange("p k n -> p (k n)"),
+                in_=w_grouped[i][:, first * HALF : last * HALF, :].rearrange("p n t -> p (n t)"),
             )
 
         def first_matmul(i):
@@ -286,26 +297,25 @@ def tile_blockresmlp_mixerblock_pb_kernel(tc, x_blocks, w1, b1, w2, b2, out):
             nc.sync.dma_start(out=out[h * P : (h + 1) * P, g * BLOCK : (g + 1) * BLOCK], in_=result[:])
 
         start_loads(-1)
+        regroup(nc.scalar.copy, 0, 0, FIRST_HALF)
+        regroup(nc.vector.tensor_copy, 0, FIRST_HALF, HALF)
+        quantise_w(0, kinds=1, first=0)
         spread_b2(0, 0, True)
         transpose_x(0)
         copy_x(0)
-        for h in range(BATCH_TILES):
-            add_x_b2(0, h)
+        add_x_b2(0, 0)
+        quantise_x(0)
+        first_matmul(0)
         b1_psum = other_psum.tile([P, P], BF16, name="b1_psum", tag="out_psum", bufs=2)
         nc.tensor.transpose(out=b1_psum[:], in_=b1_rows[:], identity=ident_bf16[:])
-        regroup_scalar(0)
-        quantise_x(0)
         nc.vector.tensor_copy(out=b1_cols[:], in_=b1_psum[:, 0 : PACK * PIECES])
+        add_x_b2(0, 1)
+        regroup_scalar(1)
+        regroup_vector(0)
+        regroup_vector(1)
+        quantise_w(0, kinds=1, first=1)
         transpose_x(1)
         spread_b2(1, 1, True)
-        regroup_vector(0)
-        regroup_scalar(1)
-        quantise_w(0)
-        first_matmul(0)
-        copy_x(1)
-        regroup_vector(1)
-        quantise_x(1)
-        start_loads(1)
 
         for s in range(PIECES + 2):
             even = s % 2 == 0
@@ -313,6 +323,8 @@ def tile_blockresmlp_mixerblock_pb_kernel(tc, x_blocks, w1, b1, w2, b2, out):
             behind = s - 1
             if s + 1 < PIECES:
                 quantise_w(s + 1)
+                if not even:
+                    quantise_x((s + 1) // 2)
                 first_matmul(s + 1)
             if not even and (s + 3) // 2 < BLOCKS:
                 transpose_x((s + 3) // 2)
@@ -321,29 +333,32 @@ def tile_blockresmlp_mixerblock_pb_kernel(tc, x_blocks, w1, b1, w2, b2, out):
                     exp_relu(s, part)
             if even and g + 1 < FIRST_SUMMED_BLOCK:
                 add_x_b2(g + 1, 0)
-            if 0 <= behind < PIECES:
-                for part in parts(behind):
-                    elu(behind, part)
             if s + 2 < PIECES:
+                if behind >= 0:
+                    elu(behind, (0, 1))
                 regroup_vector(s + 2)
                 regroup_scalar(s + 2)
                 start_loads(s + 2)
-            if FIRST_SUMMED_BLOCK <= behind // 2 < BLOCKS:
-                copy_x_b2(behind // 2, behind % 2)
-            if not even and s >= 3:
-                for h in range(BATCH_TILES):
-                    finish((s - 3) // 2, h)
-            if 0 <= behind < PIECES:
+            if FIRST_SUMMED_BLOCK <= (s + 1) // 2 < BLOCKS:
+                copy_x_b2((s + 1) // 2, (s + 1) % 2)
+            if 0 <= behind < PIECES and s + 2 >= PIECES:
                 for part in parts(behind):
+                    elu(behind, part)
                     quantise_h(behind, part)
                     for h in part:
                         second_matmul(behind, h)
+            if not even and s >= 3:
+                for h in range(BATCH_TILES):
+                    finish((s - 3) // 2, h)
+            if 0 <= behind and s + 2 < PIECES:
+                quantise_h(behind, (0, 1))
+                for h in range(BATCH_TILES):
+                    second_matmul(behind, h)
             if even and g + 1 < FIRST_SUMMED_BLOCK:
                 add_x_b2(g + 1, 1)
                 if g + 2 < FIRST_SUMMED_BLOCK:
                     spread_b2(g + 2, g + 2, True)
-            if FIRST_SUMMED_BLOCK <= g < BLOCKS:
-                sum_x_b2(g, s % 2)
-            if even and 2 <= g + 1 < BLOCKS:
+            if FIRST_SUMMED_BLOCK <= g + 1 < BLOCKS:
+                sum_x_b2(g + 1, s % 2)
+            if even and g + 1 < BLOCKS:
                 copy_x(g + 1)
-                quantise_x(g + 1)

@@ -25,6 +25,7 @@ FLOPS = 2 * BATCH * BLOCK * HIDDEN * BLOCKS * 2
 RAW_BUFS = 6
 VECTOR_W1 = 16
 SCALAR_W1 = HALF - VECTOR_W1
+RUN = 8
 HEAD_PIECES = 2
 FIRST_HALF = HALF // 2
 FIRST_SUMMED_BLOCK = 3
@@ -192,8 +193,8 @@ def tile_blockresmlp_mixerblock_pb_kernel(tc, x_blocks, w1, b1, w2, b2, out):
                     [P, 2 * HALF, PACK], BF16, name="w_grouped", tag="w_grouped", align_bytes=64
                 )
             copy(
-                out=w_grouped[i][:, first:last, :].rearrange("p (c i) t -> p c t i", i=4),
-                in_=raw_columns(i, first, last).rearrange("p t (c i) -> p c t i", i=4),
+                out=w_grouped[i][:, first:last, :].rearrange("p (c i) t -> p c t i", i=RUN),
+                in_=raw_columns(i, first, last).rearrange("p t (c i) -> p c t i", i=RUN),
             )
 
         def regroup_scalar(i):

@@ -23,9 +23,10 @@ PIECES = 2 * BLOCKS
 FLOPS = 2 * BATCH * BLOCK * HIDDEN * BLOCKS * 2
 
 RAW_BUFS = 6
-VECTOR_W1 = 16
+VECTOR_W1 = 64
 SCALAR_W1 = HALF - VECTOR_W1
 RUN = 8
+QUARTERS = 4
 HEAD_PIECES = 2
 FIRST_HALF = HALF // 2
 FIRST_SUMMED_BLOCK = 3
@@ -147,8 +148,8 @@ def tile_blockresmlp_mixerblock_pb_kernel(tc, x_blocks, w1, b1, w2, b2, out):
                 [P, PACK * BATCH], BF16, name="z_grouped", tag="z_grouped", align_bytes=64
             )
             nc.scalar.copy(
-                out=z_grouped[g][:].bitcast(F32).rearrange("p (b u) -> p b u", u=2),
-                in_=x_psum[g][:].rearrange("p u b -> p b u"),
+                out=z_grouped[g][:].bitcast(F32).rearrange("p (c i u) -> p c i u", i=QUARTERS, u=2),
+                in_=x_psum[g][:].rearrange("p u (i c) -> p c i u", i=QUARTERS),
             )
 
         def quantise_x(g):
@@ -236,34 +237,42 @@ def tile_blockresmlp_mixerblock_pb_kernel(tc, x_blocks, w1, b1, w2, b2, out):
             return slice(part[0] * P, (part[-1] + 1) * P)
 
         def exp_relu(i, part):
-            if i not in exp_and_relu:
-                exp_and_relu[i] = [
-                    act_pool.tile([P, PACK, BATCH], dtype, name=name, tag=name, bufs=3)
-                    for name, dtype in (("e", F32), ("r", BF16))
-                ]
-            for dst, func in zip(exp_and_relu[i], (ACT.Exp, ACT.Relu)):
+            whole = len(part) == BATCH_TILES
+            shape = [P, BATCH // QUARTERS, PACK, QUARTERS] if whole else [P, PACK, P]
+            exp_and_relu[(i, part)] = [
+                act_pool.tile(shape, F32, name=name, tag=name, bufs=3)
+                for name in ("e", "r")
+            ]
+            for dst, func in zip(exp_and_relu[(i, part)], (ACT.Exp, ACT.Relu)):
                 for t in range(PACK):
+                    src = h_psum[i][t // 2][:, t % 2, :]
+                    if whole:
+                        dst_t = dst[:, :, t, :]
+                        src = src.rearrange("p (c i) -> p c i", i=QUARTERS)
+                    else:
+                        first = 2 * part[0]
+                        dst_t = dst[:, t, :].rearrange("p (i c) -> p i c", i=2)
+                        src = src.rearrange("p (c i) -> p i c", i=QUARTERS)[:, first : first + 2, :]
                     nc.scalar.activation(
-                        out=dst[:, t, rows(part)],
-                        in_=h_psum[i][t // 2][:, t % 2, rows(part)],
+                        out=dst_t,
+                        in_=src,
                         func=func,
                         bias=b1_cols[:, PACK * i + t : PACK * i + t + 1],
                         scale=1.0,
                     )
 
         def elu(i, part):
-            e, r = exp_and_relu[i]
+            e, r = exp_and_relu[(i, part)]
             if i not in h_grouped:
                 h_grouped[i] = act_pool.tile(
                     [P, BATCH, PACK], BF16, name="h_grouped", tag="h_grouped", align_bytes=64
                 )
+            if len(part) == BATCH_TILES:
+                order = [e[:], r[:], h_grouped[i][:].rearrange("p (i c) t -> p c t i", i=QUARTERS)]
+            else:
+                order = [e[:].rearrange("p t b -> p b t"), r[:].rearrange("p t b -> p b t"), h_grouped[i][:, rows(part), :]]
             nc.vector.scalar_tensor_tensor(
-                out=h_grouped[i][:, rows(part), :],
-                in0=e[:, :, rows(part)].rearrange("p t b -> p b t"),
-                scalar=-1.0,
-                in1=r[:, :, rows(part)].rearrange("p t b -> p b t"),
-                op0=ALU.add,
-                op1=ALU.min,
+                out=order[2], in0=order[0], scalar=-1.0, in1=order[1], op0=ALU.add, op1=ALU.min
             )
 
         def quantise_h(i, part):

@@ -25,11 +25,13 @@ FLOPS = 2 * BATCH * BLOCK * HIDDEN * BLOCKS * 2
 RAW_BUFS = 6
 VECTOR_W1 = 64
 SCALAR_W1 = HALF - VECTOR_W1
-RUN = 8
+SCALAR_RUN = 8
+VECTOR_RUN = 4
 QUARTERS = 4
 HEAD_PIECES = 2
 FIRST_HALF = HALF // 2
 FIRST_SUMMED_BLOCK = 3
+LAST = BLOCKS - 1
 
 
 def tile_blockresmlp_mixerblock_pb_kernel(tc, x_blocks, w1, b1, w2, b2, out):
@@ -188,21 +190,21 @@ def tile_blockresmlp_mixerblock_pb_kernel(tc, x_blocks, w1, b1, w2, b2, out):
         def copy_x_b2(g, h):
             nc.scalar.copy(out=resid_tile(g)[:, h, :], in_=b2_psum[(g, h)][:])
 
-        def regroup(copy, i, first, last):
+        def regroup(copy, run, i, first, last):
             if i not in w_grouped:
                 w_grouped[i] = grouped_pool.tile(
                     [P, 2 * HALF, PACK], BF16, name="w_grouped", tag="w_grouped", align_bytes=64
                 )
             copy(
-                out=w_grouped[i][:, first:last, :].rearrange("p (c i) t -> p c t i", i=RUN),
-                in_=raw_columns(i, first, last).rearrange("p t (c i) -> p c t i", i=RUN),
+                out=w_grouped[i][:, first:last, :].rearrange("p (c i) t -> p c t i", i=run),
+                in_=raw_columns(i, first, last).rearrange("p t (c i) -> p c t i", i=run),
             )
 
         def regroup_scalar(i):
-            regroup(nc.scalar.copy, i, 0, SCALAR_W1 if i >= HEAD_PIECES else HALF)
+            regroup(nc.scalar.copy, SCALAR_RUN, i, 0, SCALAR_W1 if i >= HEAD_PIECES else HALF)
 
         def regroup_vector(i):
-            regroup(nc.vector.tensor_copy, i, SCALAR_W1 if i >= HEAD_PIECES else HALF, 2 * HALF)
+            regroup(nc.vector.tensor_copy, VECTOR_RUN, i, SCALAR_W1 if i >= HEAD_PIECES else HALF, 2 * HALF)
 
         def quantise_w(i, kinds=2, first=0):
             if i not in w_codes:
@@ -287,8 +289,11 @@ def tile_blockresmlp_mixerblock_pb_kernel(tc, x_blocks, w1, b1, w2, b2, out):
 
         def second_matmul(i, h):
             g, c = divmod(i, 2)
-            if c == 0:
+            if c == 0 and g < LAST:
                 out_psum[(g, h)] = other_psum.tile([P, BLOCK], F32, name="out_psum", tag="out_psum", bufs=2)
+            elif c == 0:
+                tag = ("x_psum", "b2_psum")[h]
+                out_psum[(g, h)] = other_psum.tile([P, BLOCK], F32, name="last_psum", tag=tag)
             nc.tensor.matmul_mx(
                 out=out_psum[(g, h)][:],
                 lhsT=h_codes[i][:, h * P : (h + 1) * P].bitcast(FP8X4),
@@ -307,21 +312,21 @@ def tile_blockresmlp_mixerblock_pb_kernel(tc, x_blocks, w1, b1, w2, b2, out):
             nc.sync.dma_start(out=out[h * P : (h + 1) * P, g * BLOCK : (g + 1) * BLOCK], in_=result[:])
 
         start_loads(-1)
-        regroup(nc.scalar.copy, 0, 0, FIRST_HALF)
-        regroup(nc.vector.tensor_copy, 0, FIRST_HALF, HALF)
+        regroup(nc.scalar.copy, SCALAR_RUN, 0, 0, FIRST_HALF)
+        regroup(nc.vector.tensor_copy, VECTOR_RUN, 0, FIRST_HALF, HALF)
         quantise_w(0, kinds=1, first=0)
         spread_b2(0, 0, True)
         transpose_x(0)
         copy_x(0)
         add_x_b2(0, 0)
         quantise_x(0)
-        first_matmul(0)
         b1_psum = other_psum.tile([P, P], BF16, name="b1_psum", tag="out_psum", bufs=2)
         nc.tensor.transpose(out=b1_psum[:], in_=b1_rows[:], identity=ident_bf16[:])
-        nc.vector.tensor_copy(out=b1_cols[:], in_=b1_psum[:, 0 : PACK * PIECES])
+        first_matmul(0)
         add_x_b2(0, 1)
         regroup_scalar(1)
         regroup_vector(0)
+        nc.vector.tensor_copy(out=b1_cols[:], in_=b1_psum[:, 0 : PACK * PIECES])
         regroup_vector(1)
         quantise_w(0, kinds=1, first=1)
         transpose_x(1)
@@ -349,21 +354,21 @@ def tile_blockresmlp_mixerblock_pb_kernel(tc, x_blocks, w1, b1, w2, b2, out):
                 regroup_vector(s + 2)
                 regroup_scalar(s + 2)
                 start_loads(s + 2)
-            if FIRST_SUMMED_BLOCK <= (s + 1) // 2 < BLOCKS:
-                copy_x_b2((s + 1) // 2, (s + 1) % 2)
-            if 0 <= behind < PIECES and s + 2 >= PIECES:
+                if behind >= 0:
+                    quantise_h(behind, (0, 1))
+                    for h in range(BATCH_TILES):
+                        second_matmul(behind, h)
+            elif behind < PIECES:
                 for part in parts(behind):
                     elu(behind, part)
                     quantise_h(behind, part)
                     for h in part:
                         second_matmul(behind, h)
+            if FIRST_SUMMED_BLOCK <= (s + 1) // 2 < BLOCKS:
+                copy_x_b2((s + 1) // 2, (s + 1) % 2)
             if not even and s >= 3:
                 for h in range(BATCH_TILES):
                     finish((s - 3) // 2, h)
-            if 0 <= behind and s + 2 < PIECES:
-                quantise_h(behind, (0, 1))
-                for h in range(BATCH_TILES):
-                    second_matmul(behind, h)
             if even and g + 1 < FIRST_SUMMED_BLOCK:
                 add_x_b2(g + 1, 1)
                 if g + 2 < FIRST_SUMMED_BLOCK:

@@ -23,11 +23,12 @@ PIECES = 2 * BLOCKS
 FLOPS = 2 * BATCH * BLOCK * HIDDEN * BLOCKS * 2
 
 RAW_BUFS = 6
-VECTOR_W1 = 64
+VECTOR_W1 = 24
 SCALAR_W1 = HALF - VECTOR_W1
 SCALAR_RUN = 8
 VECTOR_RUN = 4
 QUARTERS = 4
+GPSIMD_W1 = 160
 HEAD_PIECES = 2
 FIRST_HALF = HALF // 2
 FIRST_SUMMED_BLOCK = 3
@@ -200,8 +201,23 @@ def tile_blockresmlp_mixerblock_pb_kernel(tc, x_blocks, w1, b1, w2, b2, out):
                 in_=raw_columns(i, first, last).rearrange("p t (c i) -> p c t i", i=run),
             )
 
+        def beside_adds(i):
+            return i % 2 == 1 and i >= 5
+
         def regroup_scalar(i):
-            regroup(nc.scalar.copy, SCALAR_RUN, i, 0, SCALAR_W1 if i >= HEAD_PIECES else HALF)
+            last = SCALAR_W1 if i >= HEAD_PIECES else HALF
+            regroup(nc.scalar.copy, SCALAR_RUN, i, 0, last - GPSIMD_W1 if beside_adds(i) else last)
+
+        def regroup_gpsimd(i):
+            regroup(
+                lambda out, in_: nc.gpsimd.tensor_scalar(
+                    out=out, in0=in_, scalar1=1.0, scalar2=0.0, op0=ALU.mult, op1=ALU.add
+                ),
+                SCALAR_RUN,
+                i,
+                SCALAR_W1 - GPSIMD_W1,
+                SCALAR_W1 + SCALAR_RUN,
+            )
 
         def regroup_vector(i):
             regroup(nc.vector.tensor_copy, VECTOR_RUN, i, SCALAR_W1 if i >= HEAD_PIECES else HALF, 2 * HALF)
@@ -352,8 +368,13 @@ def tile_blockresmlp_mixerblock_pb_kernel(tc, x_blocks, w1, b1, w2, b2, out):
                 if behind >= 0:
                     elu(behind, (0, 1))
                 regroup_vector(s + 2)
+                if beside_adds(s + 2):
+                    regroup_gpsimd(s + 2)
                 regroup_scalar(s + 2)
                 start_loads(s + 2)
+                if beside_adds(s + 2):
+                    for h in range(BATCH_TILES):
+                        finish((s - 3) // 2, h)
                 if behind >= 0:
                     quantise_h(behind, (0, 1))
                     for h in range(BATCH_TILES):
@@ -361,14 +382,16 @@ def tile_blockresmlp_mixerblock_pb_kernel(tc, x_blocks, w1, b1, w2, b2, out):
             elif behind < PIECES:
                 for part in parts(behind):
                     elu(behind, part)
+                    if (s, part[0]) in ((PIECES - 1, 0), (PIECES, 0)):
+                        finish(LAST - 1, s - (PIECES - 1))
                     quantise_h(behind, part)
                     for h in part:
                         second_matmul(behind, h)
             if FIRST_SUMMED_BLOCK <= (s + 1) // 2 < BLOCKS:
                 copy_x_b2((s + 1) // 2, (s + 1) % 2)
-            if not even and s >= 3:
+            if s == PIECES + 1:
                 for h in range(BATCH_TILES):
-                    finish((s - 3) // 2, h)
+                    finish(LAST, h)
             if even and g + 1 < FIRST_SUMMED_BLOCK:
                 add_x_b2(g + 1, 1)
                 if g + 2 < FIRST_SUMMED_BLOCK:

@@ -23,10 +23,10 @@ PIECES = 2 * BLOCKS
 FLOPS = 2 * BATCH * BLOCK * HIDDEN * BLOCKS * 2
 
 RAW_BUFS = 6
-VECTOR_W1 = 24
+VECTOR_W1 = 32
 SCALAR_W1 = HALF - VECTOR_W1
 SCALAR_RUN = 8
-VECTOR_RUN = 4
+VECTOR_RUN = 8
 QUARTERS = 4
 GPSIMD_W1 = 160
 HEAD_PIECES = 2

from contextlib import ExitStack

import concourse.mybir as mybir
from concourse.masks import make_identity

F32 = mybir.dt.float32
BF16 = mybir.dt.bfloat16
U32 = mybir.dt.uint32
U8 = mybir.dt.uint8
FP8X4 = mybir.dt.float8_e4m3fn_x4
ACT = mybir.ActivationFunctionType
ALU = mybir.AluOpType

P = 128
PACK = 4
BATCH = 256
BATCH_TILES = BATCH // P
BLOCKS = 8
BLOCK = 512
HIDDEN = 1024
HALF = HIDDEN // 2
PIECES = 2 * BLOCKS
FLOPS = 2 * BATCH * BLOCK * HIDDEN * BLOCKS * 2

RAW_BUFS = 6
VECTOR_W1 = 32
SCALAR_W1 = HALF - VECTOR_W1
SCALAR_RUN = 8
VECTOR_RUN = 8
QUARTERS = 4
GPSIMD_W1 = 160
HEAD_PIECES = 2
FIRST_HALF = HALF // 2
FIRST_SUMMED_BLOCK = 3
LAST = BLOCKS - 1


def tile_blockresmlp_mixerblock_pb_kernel(tc, x_blocks, w1, b1, w2, b2, out):
    nc = tc.nc
    with ExitStack() as ctx:
        const = ctx.enter_context(tc.tile_pool(name="const", bufs=1))
        raw_pool = ctx.enter_context(tc.tile_pool(name="raw", bufs=RAW_BUFS))
        grouped_pool = ctx.enter_context(tc.tile_pool(name="grouped", bufs=3))
        codes_pool = ctx.enter_context(tc.tile_pool(name="codes", bufs=5))
        act_pool = ctx.enter_context(tc.tile_pool(name="act", bufs=2))
        out_pool = ctx.enter_context(tc.tile_pool(name="outp", bufs=3))
        hidden_psum = ctx.enter_context(tc.psum_pool(name="hidden_psum", bufs=4))
        other_psum = ctx.enter_context(tc.psum_pool(name="other_psum", bufs=1))
        ctx.enter_context(tc.manual_schedule())

        ident_f32 = const.tile([P, P], F32, name="ident_f32")
        make_identity(nc, ident_f32[:])
        ident_bf16 = const.tile([P, P], BF16, name="ident_bf16")
        make_identity(nc, ident_bf16[:])
        b2_rows = const.tile([P, BLOCK], BF16, name="b2_rows")
        nc.vector.memset(b2_rows[:], 0.0)
        b1_rows = const.tile([P, P], BF16, name="b1_rows")
        nc.vector.memset(b1_rows[64:P, :], 0.0)
        b1_cols = const.tile([P, PACK * PIECES], F32, name="b1_cols")
        dummy_in = const.tile([P, 1], F32, name="dummy_in")
        dummy_out = const.tile([P, 1], F32, name="dummy_out")
        nc.vector.memset(dummy_in[:], 0.0)
        nc.scalar.activation(out=dummy_out[:], in_=dummy_in[:], func=ACT.Exp)

        x_dram = x_blocks.rearrange("(h p) c -> p h c", p=P)
        x_sb = [const.tile([P, BATCH_TILES, BLOCK], BF16, name="x_sb%d" % g) for g in range(BLOCKS)]
        raw = {}
        head_raw = {}

        def raw_columns(i, first, last):
            if i < HEAD_PIECES:
                key = (i, first, last)
                if key not in head_raw:
                    head_raw[key] = const.tile([P, PACK, last - first], BF16, name="raw_%d_%d_%d" % key)
                return head_raw[key][:]
            if i not in raw:
                raw[i] = raw_pool.tile([P, PACK, 2 * HALF], BF16, name="raw", tag="raw")
            return raw[i][:, :, first:last]

        def load(kind, i):
            g, c = divmod(i, 2)
            if kind == "b1":
                nc.sync.dma_start(
                    out=b1_rows[0:64, :], in_=b1.rearrange("g o (m p) -> (g o m) p", p=P)
                )
            elif kind == "b2":
                nc.sync.dma_start(out=b2_rows[0:BLOCKS, :], in_=b2.rearrange("g o d -> (g o) d"))
            elif kind == "x":
                nc.sync.dma_start(out=x_sb[i][:], in_=x_dram[:, :, i * BLOCK : (i + 1) * BLOCK])
            elif kind == "w1":
                for first, last in ((0, FIRST_HALF), (FIRST_HALF, HALF)) if i == 0 else ((0, HALF),):
                    for u in range(2):
                        nc.sync.dma_start(
                            out=raw_columns(i, first, last)[:, 2 * u : 2 * u + 2, :],
                            in_=w1[g][
                                256 * u : 256 * (u + 1), c * HALF + first : c * HALF + last
                            ].rearrange("(q e) n -> q e n", e=2),
                        )
            else:
                nc.sync.dma_start(
                    out=raw_columns(i, HALF, 2 * HALF),
                    in_=w2[g][c * HALF : (c + 1) * HALF, :].rearrange("(t p) d -> p t d", p=P),
                )

        load_order = [("w1", 0), ("b2", 0), ("x", 0), ("b1", 0), ("w1", 1), ("w2", 0), ("w2", 1), ("x", 1)]
        for i in range(2, PIECES):
            load_order.append(("w1", i))
            load_order.append(("w2", i))
            if i % 2 == 0 and i // 2 + 1 < BLOCKS:
                load_order.append(("x", i // 2 + 1))
        loads_started = [0]

        def start_loads(regrouped):
            while loads_started[0] < len(load_order):
                kind, i = load_order[loads_started[0]]
                if kind in ("w1", "w2") and i - RAW_BUFS >= HEAD_PIECES and i - RAW_BUFS > regrouped:
                    break
                load(kind, i)
                loads_started[0] += 1

        x_psum = {}
        z_grouped = {}
        z_codes = {}
        z_scales = {}
        b2_psum = {}
        resid = {}
        w_grouped = {}
        w_codes = {}
        w_scales = {}
        h_psum = {}
        exp_and_relu = {}
        h_grouped = {}
        h_codes = {}
        h_scales = {}
        out_psum = {}

        def transpose_x(g):
            x_psum[g] = other_psum.tile([P, 2, BATCH], F32, name="x_psum", tag="x_psum")
            words = x_sb[g][:].rearrange("p h c -> p (h c)").bitcast(F32)
            for u in range(2):
                for h in range(BATCH_TILES):
                    first = h * (BLOCK // 2) + P * u
                    nc.tensor.transpose(
                        out=x_psum[g][:, u, h * P : (h + 1) * P],
                        in_=words[:, first : first + P],
                        identity=ident_f32[:],
                    )

        def copy_x(g):
            z_grouped[g] = act_pool.tile(
                [P, PACK * BATCH], BF16, name="z_grouped", tag="z_grouped", align_bytes=64
            )
            nc.scalar.copy(
                out=z_grouped[g][:].bitcast(F32).rearrange("p (c i u) -> p c i u", i=QUARTERS, u=2),
                in_=x_psum[g][:].rearrange("p u (i c) -> p c i u", i=QUARTERS),
            )

        def quantise_x(g):
            z_codes[g] = act_pool.tile([P, BATCH], U32, name="z_codes", tag="z_codes", bufs=3, align_bytes=64)
            z_scales[g] = act_pool.tile([P, BATCH], U8, name="z_scales", tag="z_scales", bufs=3, align_bytes=64)
            nc.vector.quantize_mx(
                out=z_codes[g][:].bitcast(FP8X4), scales=z_scales[g][:], in_=z_grouped[g][:]
            )

        def spread_b2(key, g, stop):
            b2_psum[key] = other_psum.tile([P, BLOCK], F32, name="b2_psum", tag="b2_psum")
            nc.tensor.matmul(
                out=b2_psum[key][:],
                lhsT=ident_bf16[:, g : g + 1].to_broadcast([P, P]),
                rhs=b2_rows[:],
                start=True,
                stop=stop,
            )

        def resid_tile(g):
            if g not in resid:
                resid[g] = out_pool.tile([P, BATCH_TILES, BLOCK], F32, name="resid", tag="resid")
            return resid[g]

        def add_x_b2(g, h):
            nc.vector.tensor_tensor(
                out=resid_tile(g)[:, h, :], in0=b2_psum[g][:], in1=x_sb[g][:, h, :], op=ALU.add
            )

        def sum_x_b2(g, h):
            spread_b2((g, h), g, False)
            nc.tensor.matmul(
                out=b2_psum[(g, h)][:], lhsT=ident_bf16[:], rhs=x_sb[g][:, h, :], start=False, stop=True
            )

        def copy_x_b2(g, h):
            nc.scalar.copy(out=resid_tile(g)[:, h, :], in_=b2_psum[(g, h)][:])

        def regroup(copy, run, i, first, last):
            if i not in w_grouped:
                w_grouped[i] = grouped_pool.tile(
                    [P, 2 * HALF, PACK], BF16, name="w_grouped", tag="w_grouped", align_bytes=64
                )
            copy(
                out=w_grouped[i][:, first:last, :].rearrange("p (c i) t -> p c t i", i=run),
                in_=raw_columns(i, first, last).rearrange("p t (c i) -> p c t i", i=run),
            )

        def beside_adds(i):
            return i % 2 == 1 and i >= 5

        def regroup_scalar(i):
            last = SCALAR_W1 if i >= HEAD_PIECES else HALF
            regroup(nc.scalar.copy, SCALAR_RUN, i, 0, last - GPSIMD_W1 if beside_adds(i) else last)

        def regroup_gpsimd(i):
            regroup(
                lambda out, in_: nc.gpsimd.tensor_scalar(
                    out=out, in0=in_, scalar1=1.0, scalar2=0.0, op0=ALU.mult, op1=ALU.add
                ),
                SCALAR_RUN,
                i,
                SCALAR_W1 - GPSIMD_W1,
                SCALAR_W1 + SCALAR_RUN,
            )

        def regroup_vector(i):
            regroup(nc.vector.tensor_copy, VECTOR_RUN, i, SCALAR_W1 if i >= HEAD_PIECES else HALF, 2 * HALF)

        def quantise_w(i, kinds=2, first=0):
            if i not in w_codes:
                w_codes[i] = codes_pool.tile([P, 2, HALF], U32, name="w_codes", tag="w_codes", align_bytes=64)
                w_scales[i] = codes_pool.tile([P, 2, HALF], U8, name="w_scales", tag="w_scales", align_bytes=64)
            last = first + kinds
            nc.vector.quantize_mx(
                out=w_codes[i][:, first:last, :].rearrange("p k n -> p (k n)").bitcast(FP8X4),
                scales=w_scales[i][:, first:last, :].rearrange("p k n -> p (k n)"),
                in_=w_grouped[i][:, first * HALF : last * HALF, :].rearrange("p n t -> p (n t)"),
            )

        def first_matmul(i):
            h_psum[i] = [
                hidden_psum.tile([P, 2, BATCH], F32, name="h_psum%d" % k, tag="h_psum") for k in range(2)
            ]
            for t in range(PACK):
                nc.tensor.matmul_mx(
                    out=h_psum[i][t // 2][:, t % 2, :],
                    lhsT=w_codes[i][:, 0, t * P : (t + 1) * P].bitcast(FP8X4),
                    lhsT_scale=w_scales[i][:, 0, t * P : (t + 1) * P],
                    rhs=z_codes[i // 2][:].bitcast(FP8X4),
                    rhs_scale=z_scales[i // 2][:],
                    start=True,
                    stop=True,
                )

        def parts(i):
            return ((0,), (1,)) if i == PIECES - 1 else ((0, 1),)

        def rows(part):
            return slice(part[0] * P, (part[-1] + 1) * P)

        def exp_relu(i, part):
            whole = len(part) == BATCH_TILES
            shape = [P, BATCH // QUARTERS, PACK, QUARTERS] if whole else [P, PACK, P]
            exp_and_relu[(i, part)] = [
                act_pool.tile(shape, F32, name=name, tag=name, bufs=3)
                for name in ("e", "r")
            ]
            for dst, func in zip(exp_and_relu[(i, part)], (ACT.Exp, ACT.Relu)):
                for t in range(PACK):
                    src = h_psum[i][t // 2][:, t % 2, :]
                    if whole:
                        dst_t = dst[:, :, t, :]
                        src = src.rearrange("p (c i) -> p c i", i=QUARTERS)
                    else:
                        first = 2 * part[0]
                        dst_t = dst[:, t, :].rearrange("p (i c) -> p i c", i=2)
                        src = src.rearrange("p (c i) -> p i c", i=QUARTERS)[:, first : first + 2, :]
                    nc.scalar.activation(
                        out=dst_t,
                        in_=src,
                        func=func,
                        bias=b1_cols[:, PACK * i + t : PACK * i + t + 1],
                        scale=1.0,
                    )

        def elu(i, part):
            e, r = exp_and_relu[(i, part)]
            if i not in h_grouped:
                h_grouped[i] = act_pool.tile(
                    [P, BATCH, PACK], BF16, name="h_grouped", tag="h_grouped", align_bytes=64
                )
            if len(part) == BATCH_TILES:
                order = [e[:], r[:], h_grouped[i][:].rearrange("p (i c) t -> p c t i", i=QUARTERS)]
            else:
                order = [e[:].rearrange("p t b -> p b t"), r[:].rearrange("p t b -> p b t"), h_grouped[i][:, rows(part), :]]
            nc.vector.scalar_tensor_tensor(
                out=order[2], in0=order[0], scalar=-1.0, in1=order[1], op0=ALU.add, op1=ALU.min
            )

        def quantise_h(i, part):
            if i not in h_codes:
                h_codes[i] = act_pool.tile([P, BATCH], U32, name="h_codes", tag="h_codes", bufs=4, align_bytes=64)
                h_scales[i] = act_pool.tile([P, BATCH], U8, name="h_scales", tag="h_scales", bufs=4, align_bytes=64)
            nc.vector.quantize_mx(
                out=h_codes[i][:, rows(part)].bitcast(FP8X4),
                scales=h_scales[i][:, rows(part)],
                in_=h_grouped[i][:, rows(part), :].rearrange("p b t -> p (b t)"),
            )

        def second_matmul(i, h):
            g, c = divmod(i, 2)
            if c == 0 and g < LAST:
                out_psum[(g, h)] = other_psum.tile([P, BLOCK], F32, name="out_psum", tag="out_psum", bufs=2)
            elif c == 0:
                tag = ("x_psum", "b2_psum")[h]
                out_psum[(g, h)] = other_psum.tile([P, BLOCK], F32, name="last_psum", tag=tag)
            nc.tensor.matmul_mx(
                out=out_psum[(g, h)][:],
                lhsT=h_codes[i][:, h * P : (h + 1) * P].bitcast(FP8X4),
                lhsT_scale=h_scales[i][:, h * P : (h + 1) * P],
                rhs=w_codes[i][:, 1, :].bitcast(FP8X4),
                rhs_scale=w_scales[i][:, 1, :],
                start=(c == 0),
                stop=(c == 1),
            )

        def finish(g, h):
            result = out_pool.tile([P, BLOCK], F32, name="result", tag="result", bufs=4)
            nc.vector.tensor_tensor(
                out=result[:], in0=out_psum[(g, h)][:], in1=resid[g][:, h, :], op=ALU.add
            )
            nc.sync.dma_start(out=out[h * P : (h + 1) * P, g * BLOCK : (g + 1) * BLOCK], in_=result[:])

        start_loads(-1)
        regroup(nc.scalar.copy, SCALAR_RUN, 0, 0, FIRST_HALF)
        regroup(nc.vector.tensor_copy, VECTOR_RUN, 0, FIRST_HALF, HALF)
        quantise_w(0, kinds=1, first=0)
        spread_b2(0, 0, True)
        transpose_x(0)
        copy_x(0)
        add_x_b2(0, 0)
        quantise_x(0)
        b1_psum = other_psum.tile([P, P], BF16, name="b1_psum", tag="out_psum", bufs=2)
        nc.tensor.transpose(out=b1_psum[:], in_=b1_rows[:], identity=ident_bf16[:])
        first_matmul(0)
        add_x_b2(0, 1)
        regroup_scalar(1)
        regroup_vector(0)
        nc.vector.tensor_copy(out=b1_cols[:], in_=b1_psum[:, 0 : PACK * PIECES])
        regroup_vector(1)
        quantise_w(0, kinds=1, first=1)
        transpose_x(1)
        spread_b2(1, 1, True)

        for s in range(PIECES + 2):
            even = s % 2 == 0
            g = s // 2
            behind = s - 1
            if s + 1 < PIECES:
                quantise_w(s + 1)
                if not even:
                    quantise_x((s + 1) // 2)
                first_matmul(s + 1)
            if not even and (s + 3) // 2 < BLOCKS:
                transpose_x((s + 3) // 2)
            if s < PIECES:
                for part in parts(s):
                    exp_relu(s, part)
            if even and g + 1 < FIRST_SUMMED_BLOCK:
                add_x_b2(g + 1, 0)
            if s + 2 < PIECES:
                if behind >= 0:
                    elu(behind, (0, 1))
                regroup_vector(s + 2)
                if beside_adds(s + 2):
                    regroup_gpsimd(s + 2)
                regroup_scalar(s + 2)
                start_loads(s + 2)
                if beside_adds(s + 2):
                    for h in range(BATCH_TILES):
                        finish((s - 3) // 2, h)
                if behind >= 0:
                    quantise_h(behind, (0, 1))
                    for h in range(BATCH_TILES):
                        second_matmul(behind, h)
            elif behind < PIECES:
                for part in parts(behind):
                    elu(behind, part)
                    if (s, part[0]) in ((PIECES - 1, 0), (PIECES, 0)):
                        finish(LAST - 1, s - (PIECES - 1))
                    quantise_h(behind, part)
                    for h in part:
                        second_matmul(behind, h)
            if FIRST_SUMMED_BLOCK <= (s + 1) // 2 < BLOCKS:
                copy_x_b2((s + 1) // 2, (s + 1) % 2)
            if s == PIECES + 1:
                for h in range(BATCH_TILES):
                    finish(LAST, h)
            if even and g + 1 < FIRST_SUMMED_BLOCK:
                add_x_b2(g + 1, 1)
                if g + 2 < FIRST_SUMMED_BLOCK:
                    spread_b2(g + 2, g + 2, True)
            if FIRST_SUMMED_BLOCK <= g + 1 < BLOCKS:
                sum_x_b2(g + 1, s % 2)
            if even and g + 1 < BLOCKS:
                copy_x(g + 1)
